import numpy as np
import ml_dtypes


def mxq(x, axis, fmt="e4m3"):
    dtype, down = {"e4m3": (ml_dtypes.float8_e4m3fn, 7), "e5m2": (ml_dtypes.float8_e5m2, 14)}[fmt]
    v = np.moveaxis(np.asarray(x, np.float32).astype(ml_dtypes.bfloat16).astype(np.float64), axis, -1)
    blocks = v.reshape(v.shape[:-1] + (-1, 32))
    amax = np.abs(blocks).max(-1, keepdims=True)
    byte = np.maximum(np.where(amax > 0, np.frexp(amax)[1] - 1 + 127, 0) - down, 1)
    scale = np.exp2(byte - 127.0)
    codes = (blocks / scale).astype(np.float32).astype(dtype).astype(np.float64)
    return np.moveaxis((codes * scale).reshape(v.shape), -1, axis)


WIDE = False


def mx_kscale(k):
    if not WIDE:
        return np.ones(k)
    levels = np.array([10, -10, 5, -5, 0])
    if k % 512:
        return np.exp2(np.random.permutation(np.resize(levels, k // 32))).repeat(32)
    a = np.empty((k // 512, 16))
    for p in range(k // 512):
        a[p, :8] = np.random.permutation(np.resize(levels, 8))
        for g in range(8):
            far = levels[np.abs(levels - a[p, g]) >= 10]
            a[p, g + 8] = far[np.random.randint(len(far))]
    return np.exp2(a.ravel()).repeat(32)


BF16 = ml_dtypes.bfloat16


def bf(x):
    return np.asarray(x, np.float32).astype(BF16)


def f64(x):
    return np.asarray(x).astype(np.float64)


B, C, HH, WW, M, L, G, HID = 4, 3072, 64, 64, 256, 512, 256, 1024
N = HH * WW
ITERS = 3
DUST = 1.0


def lse(a, axis):
    top = a.max(axis=axis, keepdims=True)
    return np.log(np.exp(a - top).sum(axis=axis)) + np.squeeze(top, axis=axis)


def setup_inputs():
    s, t = mx_kscale(C), mx_kscale(HID)
    return {
        "x": bf(np.random.standard_normal((B, C, HH, WW)) * s[None, :, None, None]),
        "Ws1": bf(np.random.standard_normal((HID, C)) / np.sqrt(C) / s[None, :] * t[:, None]),
        "bs1": bf(np.random.standard_normal(HID) * 0.3 * t),
        "Ws2": bf(np.random.standard_normal((M, HID)) * 2.0 / np.sqrt(HID) / t[None, :]),
    }


def reference(x, Ws1, bs1, Ws2):
    xf = f64(x).reshape(B, C, N)
    hs = np.maximum((mxq(f64(Ws1), 1, "e4m3") @ mxq(xf, 1, "e4m3")) + f64(bs1)[None, :, None], 0.0)
    p = mxq(f64(Ws2), 1, "e4m3") @ mxq(hs, 1, "e4m3")
    norm = -np.log(M + N)
    log_mu = np.concatenate([np.full(M, norm), np.full(1, np.log(N) + norm)])
    log_nu = np.full(N, norm)
    Z = np.concatenate([p, np.full((B, 1, N), DUST)], axis=1)
    u = np.zeros((B, M + 1))
    v = np.zeros((B, N))
    for _ in range(ITERS):
        u = log_mu[None] - lse(Z + v[:, None, :], 2)
        v = log_nu[None] - lse(Z + u[:, :, None], 1)
    return np.exp(Z + u[:, :, None] + v[:, None, :] - norm)[:, :-1, :]

@@ -1,0 +1,396 @@
+from contextlib import ExitStack
+
+import concourse.mybir as mybir
+from concourse.masks import make_identity
+
+B, C, NPIX, HID, M = 4, 3072, 4096, 1024, 256
+FLOPS = 2 * B * NPIX * (HID * C + M * HID)
+
+F32 = mybir.dt.float32
+BF16 = mybir.dt.bfloat16
+U32 = mybir.dt.uint32
+U8 = mybir.dt.uint8
+FP8X4 = mybir.dt.float8_e4m3fn_x4
+ALU = mybir.AluOpType
+ACT = mybir.ActivationFunctionType
+AX = mybir.AxisListType
+
+P = 128
+NCH = 512
+CPI = NPIX // NCH
+NQ = B * CPI
+KP1 = C // 512
+KP2 = HID // 512
+NT = NPIX // P
+NACC = 4
+S_BUSY = ((), (3, 4, 5), (0, 1, 2, 3, 4, 5), (0, 1, 2, 3, 4, 5), (0, 1, 2, 3, 4, 5), (0, 1, 2, 3, 4, 5), (0, 1, 2), ())
+S_IDLE = (1, 3, 5)
+SLOTS = 64
+PHASES = ((0, 10), (10, 50), (50, 62))
+
+
+def tile_salad_pa_l_kernel(tc, x, Ws1, bs1, Ws2, out):
+    nc = tc.nc
+    xv = x.rearrange("b c h w -> b c (h w)")
+
+    with ExitStack() as ctx:
+        const = ctx.enter_context(tc.tile_pool(name="const", bufs=1))
+        xrp = ctx.enter_context(tc.tile_pool(name="xrp", bufs=8))
+        xgp = ctx.enter_context(tc.tile_pool(name="xgp", bufs=3))
+        xcp = ctx.enter_context(tc.tile_pool(name="xcp", bufs=12))
+        hsp = ctx.enter_context(tc.tile_pool(name="hsp", bufs=2))
+        small = ctx.enter_context(tc.tile_pool(name="small", bufs=2))
+        ps1 = ctx.enter_context(tc.psum_pool(name="ps1", bufs=4))
+        ps2 = ctx.enter_context(tc.psum_pool(name="ps2", bufs=2))
+        pstr = ctx.enter_context(tc.psum_pool(name="pstr", bufs=2))
+
+        ident = const.tile([P, P], F32, name="ident")
+        make_identity(nc, ident[:])
+        ones = const.tile([P, P], F32, name="ones")
+        nc.vector.memset(ones[:], 1.0)
+        warm = const.tile([P, 1], F32, name="warm")
+        nc.scalar.activation(out=warm[:], in_=ones[:, 0:1], func=ACT.Exp)
+        b1 = const.tile([P, 2, 4], BF16, name="b1")
+        nc.sync.dma_start(out=b1[:], in_=bs1.rearrange("(g p t) -> p g t", g=2, t=4))
+        w1c = const.tile([P, 8, KP1 * P], U32, name="w1c", align_bytes=64)
+        w1s = const.tile([P, 8, KP1 * P], U8, name="w1s", align_bytes=64)
+        w2c = const.tile([P, 2, KP2 * P], U32, name="w2c", align_bytes=64)
+        w2s = const.tile([P, 2, KP2 * P], U8, name="w2s", align_bytes=64)
+        accs = []
+        for k in range(NACC):
+            acc = const.tile([P, M + 1], F32, name="acc%d" % k)
+            nc.vector.memset(acc[:], 0.0)
+            accs.append(acc)
+        junk = const.tile([P, M], F32, name="junk")
+        junk32 = const.tile([P, NT], F32, name="junk32")
+
+        xraw = {}
+        xgrp = {}
+        xcod = {}
+
+        def load(q):
+            b, c = divmod(q, CPI)
+            for g in range(KP1):
+                t = xrp.tile([P, 4, NCH], BF16, name="xraw", tag="xraw")
+                nc.sync.dma_start(
+                    out=t[:],
+                    in_=xv[b, 512 * g : 512 * (g + 1), NCH * c : NCH * (c + 1)].rearrange("(p j) n -> p j n", j=4),
+                )
+                xraw[(q, g)] = t
+
+        def inter(q, g, share):
+            src = xraw.pop((q, g))
+            t = xgp.tile([P, NCH, 4], BF16, name="xgrp", tag="xgrp", align_bytes=64)
+            if g in share:
+                nc.scalar.copy(out=t[:], in_=src[:].rearrange("p j n -> p n j"))
+            else:
+                nc.vector.tensor_copy(out=t[:], in_=src[:].rearrange("p j n -> p n j"))
+            xgrp[(q, g)] = t
+
+        def quant(q, g):
+            src = xgrp.pop((q, g))
+            cod = xcp.tile([P, NCH], U32, name="xcod", tag="xcod", align_bytes=64)
+            sca = xcp.tile([P, NCH], U8, name="xsca", tag="xsca", align_bytes=64)
+            nc.vector.quantize_mx(out=cod[:].bitcast(FP8X4), scales=sca[:], in_=src[:].rearrange("p n j -> p (n j)"))
+            xcod[(q, g)] = (cod, sca)
+
+        def turn_weights(head, rows, passes, cod, sca, eng0):
+            words = rows[:].bitcast(F32)
+            grp = head.tile([P, KP1, P, 4], BF16, name="wgrp", tag="wgrp", bufs=2, align_bytes=64)
+            gw = grp[:].bitcast(F32)
+            for gp in range(passes // 2):
+                bank = pstr.tile([P, 2, 2, P], F32, name="wbank", tag="tr")
+                for g2 in range(2):
+                    g = 2 * gp + g2
+                    for u in range(2):
+                        nc.tensor.transpose(bank[:, g2, u, :], words[:, 256 * g + u : 256 * (g + 1) : 2], ident[:])
+                if (gp + eng0) % 2 == 0:
+                    nc.vector.tensor_copy(out=gw[:, 2 * gp : 2 * gp + 2, :, :], in_=bank[:].rearrange("p g u m -> p g m u"))
+                else:
+                    nc.scalar.copy(out=gw[:, 2 * gp : 2 * gp + 2, :, :], in_=bank[:].rearrange("p g u m -> p g m u"))
+            flat = grp[:].rearrange("p g m k -> p (g m k)")
+            lo = 0
+            for width in ((2048, 1024) if passes == 6 else (1024,)):
+                nc.vector.quantize_mx(
+                    out=cod[:, lo // 4 : (lo + width) // 4].bitcast(FP8X4),
+                    scales=sca[:, lo // 4 : (lo + width) // 4],
+                    in_=flat[:, lo : lo + width],
+                )
+                lo += width
+
+        w1v = Ws1.rearrange("(g m t) k -> g t m k", g=2, t=4)
+        with tc.tile_pool(name="head", bufs=2) as head:
+            for j in range(8):
+                rows = head.tile([P, C], BF16, name="wrow", tag="wrow", bufs=3)
+                nc.sync.dma_start(out=rows[:], in_=w1v[j // 4, j % 4])
+                turn_weights(head, rows, KP1, w1c[:, j, :], w1s[:, j, :], j)
+                if j == 1:
+                    load(0)
+            for h in range(2):
+                rows2 = head.tile([P, HID], BF16, name="wrow2", tag="wrow2", bufs=2)
+                nc.sync.dma_start(out=rows2[:], in_=Ws2[P * h : P * (h + 1), :])
+                turn_weights(head, rows2, KP2, w2c[:, h, :], w2s[:, h, :], h)
+
+        pp = ctx.enter_context(tc.tile_pool(name="pp", bufs=20))
+        etp = ctx.enter_context(tc.tile_pool(name="etp", bufs=1))
+        xtp = ctx.enter_context(tc.tile_pool(name="xtp", bufs=8))
+        outp = ctx.enter_context(tc.tile_pool(name="outp", bufs=3))
+
+        hscod = {}
+        pend = []
+
+        def quant_hs():
+            q, g, grp = pend.pop(0)
+            cod = hsp.tile([P, NCH], U32, name="hcod", tag="hcod", bufs=4, align_bytes=64)
+            sca = hsp.tile([P, NCH], U8, name="hsca", tag="hsca", bufs=4, align_bytes=64)
+            nc.vector.quantize_mx(out=cod[:].bitcast(FP8X4), scales=sca[:], in_=grp[:].rearrange("p n j -> p (n j)"))
+            hscod[(q, g)] = (cod, sca)
+
+        def stage1(q, share, woven):
+            raw = None
+            for j in range(8):
+                g2, t = divmod(j, 4)
+                if q + 1 < NQ and j < KP1:
+                    inter(q + 1, j, share)
+                if q + 1 < NQ and 1 <= j <= KP1:
+                    quant(q + 1, j - 1)
+                if pend and t == 1:
+                    quant_hs()
+                acc = ps1.tile([P, NCH], F32, name="s1", tag="s1")
+                for g in range(KP1):
+                    cod, sca = xcod[(q, g)]
+                    nc.tensor.matmul_mx(
+                        out=acc[:],
+                        lhsT=w1c[:, j, P * g : P * (g + 1)].bitcast(FP8X4),
+                        lhsT_scale=w1s[:, j, P * g : P * (g + 1)],
+                        rhs=cod[:].bitcast(FP8X4),
+                        rhs_scale=sca[:],
+                        start=(g == 0),
+                        stop=(g == KP1 - 1),
+                    )
+                if t == 0:
+                    raw = hsp.tile([P, 4, NCH], BF16, name="hraw", tag="hraw", bufs=3)
+                nc.scalar.activation(out=raw[:, t, :], in_=acc[:], func=ACT.Relu, bias=b1[:, g2, t : t + 1], scale=1.0)
+                if t == 3:
+                    grp = hsp.tile([P, NCH, 4], BF16, name="hgrp", tag="hgrp", bufs=2, align_bytes=64)
+                    nc.vector.tensor_copy(out=grp[:], in_=raw[:].rearrange("p j n -> p n j"))
+                    pend.append((q, g2, grp))
+                for step in woven.pop((q % CPI) * 8 + j, ()):
+                    step()
+            for g in range(KP1):
+                xcod.pop((q, g))
+
+        def stage2(q, pt, mx):
+            c = q % CPI
+            while pend:
+                quant_hs()
+            for h in range(2):
+                acc = ps2.tile([P, NCH], F32, name="s2", tag="s2")
+                for g in range(KP2):
+                    cod, sca = hscod[(q, g)]
+                    nc.tensor.matmul_mx(
+                        out=acc[:],
+                        lhsT=w2c[:, h, P * g : P * (g + 1)].bitcast(FP8X4),
+                        lhsT_scale=w2s[:, h, P * g : P * (g + 1)],
+                        rhs=cod[:].bitcast(FP8X4),
+                        rhs_scale=sca[:],
+                        start=(g == 0),
+                        stop=(g == KP2 - 1),
+                    )
+                t = pp.tile([P, NCH], F32, name="pt", tag="pt")
+                nc.vector.tensor_scalar(
+                    out=t[:], in0=acc[:], scalar1=1.0, scalar2=None, op0=ALU.mult, op1=ALU.max,
+                    accum_out=mx[:, CPI * h + c : CPI * h + c + 1],
+                )
+                pt[(h, c)] = t
+            for g in range(KP2):
+                hscod.pop((q, g))
+
+        def sinkhorn_steps(b, pt, mx, last):
+            s = {}
+
+            def shift():
+                m2 = small.tile([P, 2], F32, name="m2", tag="m2")
+                nc.vector.tensor_reduce(out=m2[:], in_=mx[:].rearrange("p (h c) -> p h c", h=2), axis=AX.X, op=ALU.max)
+                negm = small.tile([P, 2], F32, name="negm", tag="negm")
+                nc.vector.tensor_scalar(out=negm[:], in0=m2[:], scalar1=-1.0, scalar2=None, op0=ALU.mult)
+                s["negm"] = negm
+                s["r1"] = small.tile([P, 2 * CPI], F32, name="r1", tag="r1")
+                s["et"] = etp.tile([P, NT, M], F32, name="et", tag="et")
+
+            def exps(c):
+                for h in range(2):
+                    nc.scalar.activation(
+                        out=pt[(h, c)][:], in_=pt[(h, c)][:], func=ACT.Exp, bias=s["negm"][:, h : h + 1], scale=1.0,
+                        accum_out=s["r1"][:, CPI * h + c : CPI * h + c + 1],
+                    )
+
+            def turn(c):
+                et = s["et"]
+                banks = []
+                for half in range(2):
+                    bank = pstr.tile([P, 2, 2, P], F32, name="ebank", tag="tr")
+                    for tt in range(2):
+                        for h in range(2):
+                            lo = P * (2 * half + tt)
+                            nc.tensor.transpose(bank[:, tt, h, :], pt[(h, c)][:, lo : lo + P], ident[:])
+                    banks.append(bank)
+                for half in range(2):
+                    t0 = 4 * c + 2 * half
+                    if last and half == 0:
+                        nc.vector.tensor_copy(out=et[:, t0 : t0 + 2, :], in_=banks[half][:].rearrange("p t h i -> p t (h i)"))
+                    else:
+                        nc.scalar.copy(out=et[:, t0 : t0 + 2, :], in_=banks[half][:].rearrange("p t h i -> p t (h i)"))
+
+            def first_a():
+                rc = small.tile([P, 2], F32, name="rc", tag="rc")
+                nc.vector.tensor_reduce(out=rc[:], in_=s["r1"][:].rearrange("p (h c) -> p h c", h=2), axis=AX.X, op=ALU.add)
+                rb = pstr.tile([P, NCH], F32, name="rb", tag="tr")
+                for h in range(2):
+                    nc.tensor.matmul(
+                        rb[:, P * h : P * (h + 1)], lhsT=rc[:, h : h + 1].to_broadcast([P, P]), rhs=ident[:],
+                        start=True, stop=True,
+                    )
+                abc = small.tile([P, M + 1], F32, name="abc", tag="abc")
+                nc.vector.reciprocal(out=abc[:, 0:M], in_=rb[:, 0:M])
+                nc.vector.memset(abc[:, M : M + 1], 1.0)
+                s["abc"] = abc
+
+            def col_part(t0):
+                if t0 == 0:
+                    s["cc"] = small.tile([P, NT], F32, name="cc", tag="cc")
+                for t in range(t0, t0 + 4):
+                    nc.vector.scalar_tensor_tensor(
+                        out=junk[:], in0=s["et"][:, t, :], scalar=1.0, in1=s["abc"][:, 0:M], op0=ALU.mult, op1=ALU.mult,
+                        accum_out=s["cc"][:, t : t + 1],
+                    )
+
+            def col_end():
+                cd = small.tile([P, NT], F32, name="cd", tag="cd")
+                nc.vector.tensor_scalar(out=cd[:], in0=s["cc"][:], scalar1=s["abc"][:, M : M + 1], scalar2=None, op0=ALU.add)
+                bb = small.tile([P, NT], F32, name="bb", tag="bb")
+                nc.vector.reciprocal(out=bb[:], in_=cd[:])
+                s["bb"] = bb
+
+            def row_part(t0):
+                et, bb = s["et"], s["bb"]
+                if t0 == 0:
+                    nc.vector.tensor_scalar(
+                        out=junk32[:], in0=bb[:], scalar1=1.0 / NPIX, scalar2=None, op0=ALU.mult, op1=ALU.add,
+                        accum_out=accs[0][:, M : M + 1],
+                    )
+                for t in range(t0, t0 + 4):
+                    acc = accs[t % NACC]
+                    if t < NACC:
+                        nc.vector.tensor_scalar(
+                            out=acc[:, 0:M], in0=et[:, t, :], scalar1=bb[:, t : t + 1], scalar2=None, op0=ALU.mult
+                        )
+                    else:
+                        nc.vector.scalar_tensor_tensor(
+                            out=acc[:, 0:M], in0=et[:, t, :], scalar=bb[:, t : t + 1], in1=acc[:, 0:M],
+                            op0=ALU.mult, op1=ALU.add,
+                        )
+
+            def row_end():
+                rb = pstr.tile([P, NCH], F32, name="rb", tag="tr")
+                for k in range(NACC):
+                    nc.tensor.matmul(
+                        rb[:, 0 : M + 1], lhsT=ones[:], rhs=accs[k][:], start=(k == 0), stop=(k == NACC - 1)
+                    )
+                abc = small.tile([P, M + 1], F32, name="abc", tag="abc")
+                nc.vector.reciprocal(out=abc[:], in_=rb[:, 0 : M + 1])
+                s["abc"] = abc
+
+            def a_column():
+                ab = pstr.tile([P, NCH], F32, name="ab", tag="tr")
+                acol = small.tile([P, 2], F32, name="acol", tag="acol")
+                for h in range(2):
+                    nc.tensor.transpose(ab[:, P * h : P * (h + 1)], s["abc"][:, P * h : P * (h + 1)], ident[:])
+                for h in range(2):
+                    nc.vector.tensor_copy(out=acol[:, h : h + 1], in_=ab[:, P * h : P * h + 1])
+                s["acol"] = acol
+
+            def scale_b(c):
+                xts = []
+                for t in range(4 * c, 4 * c + 4):
+                    xt = xtp.tile([P, M], F32, name="xt", tag="xt")
+                    if last:
+                        nc.vector.tensor_scalar(
+                            out=xt[:], in0=s["et"][:, t, :], scalar1=s["bb"][:, t : t + 1], scalar2=None, op0=ALU.mult
+                        )
+                    else:
+                        nc.scalar.activation(out=xt[:], in_=s["et"][:, t, :], func=ACT.Copy, scale=s["bb"][:, t : t + 1])
+                    xts.append(xt)
+                s[("xt", c)] = xts
+
+            def store(c):
+                xts = s.pop(("xt", c))
+                banks = []
+                for h in range(2):
+                    ob = pstr.tile([P, 4, P], F32, name="ob", tag="tr")
+                    for tt in range(4):
+                        nc.tensor.transpose(ob[:, tt, :], xts[tt][:, P * h : P * (h + 1)], ident[:])
+                    banks.append(ob)
+                for h in range(2):
+                    osb = outp.tile([P, NCH], F32, name="osb", tag="osb")
+                    nc.scalar.activation(
+                        out=osb[:], in_=banks[h][:].rearrange("p t n -> p (t n)"), func=ACT.Copy, scale=s["acol"][:, h : h + 1]
+                    )
+                    nc.gpsimd.dma_start(out=out[b, P * h : P * (h + 1), NCH * c : NCH * (c + 1)], in_=osb[:])
+
+            def bind(f, arg):
+                return lambda: f(arg)
+
+            prep = [shift, bind(exps, 0)]
+            for c in range(1, CPI):
+                prep.append(bind(exps, c))
+                prep.append(bind(turn, c - 1))
+            prep.append(first_a)
+            prep.append(bind(turn, CPI - 1))
+            sweeps = []
+            for it in range(3):
+                for t0 in range(0, NT, 4):
+                    sweeps.append(bind(col_part, t0))
+                sweeps.append(col_end)
+                if it < 2:
+                    for t0 in range(0, NT, 4):
+                        sweeps.append(bind(row_part, t0))
+                    sweeps.append(row_end)
+            fin = [a_column, bind(scale_b, 0)]
+            for c in range(1, CPI):
+                fin.append(bind(scale_b, c))
+                fin.append(bind(store, c - 1))
+            fin.append(bind(store, CPI - 1))
+            return (prep, sweeps, fin)
+
+        def weave(lists):
+            woven = {}
+            for steps, (lo, hi) in zip(lists, PHASES):
+                for i, step in enumerate(steps):
+                    slot = lo + (i * (hi - lo)) // len(steps)
+                    woven[slot] = woven.get(slot, []) + [step]
+            return woven
+
+        load(1)
+        for g in range(KP1):
+            inter(0, g, S_IDLE)
+            quant(0, g)
+        woven = {}
+        pt, mx = {}, None
+        for q in range(NQ):
+            b, c = divmod(q, CPI)
+            if c == 0:
+                pt = {}
+                mx = small.tile([P, 2 * CPI], F32, name="mx", tag="mx")
+            if q + 2 < NQ:
+                load(q + 2)
+            stage1(q, S_BUSY[c] if b > 0 else S_IDLE, woven)
+            stage2(q, pt, mx)
+            if c == CPI - 1:
+                lists = sinkhorn_steps(b, pt, mx, b == B - 1)
+                if b < B - 1:
+                    woven = weave(lists)
+                else:
+                    for steps in lists:
+                        for step in steps:
+                            step()

@@ -23,10 +23,11 @@ KP1 = C // 512
 KP2 = HID // 512
 NT = NPIX // P
 NACC = 4
-S_BUSY = ((), (3, 4, 5), (0, 1, 2, 3, 4, 5), (0, 1, 2, 3, 4, 5), (0, 1, 2, 3, 4, 5), (0, 1, 2, 3, 4, 5), (0, 1, 2), ())
-S_IDLE = (1, 3, 5)
-SLOTS = 64
-PHASES = ((0, 10), (10, 50), (50, 62))
+LAG = 3
+PHASES = ((4, 13), (13, 59), (59, 68))
+V_IN_SWEEPS = (29, 45, 53)
+TAIL_ROW_PE = 0
+TAIL_COL_PE = 0
 
 
 def tile_salad_pa_l_kernel(tc, x, Ws1, bs1, Ws2, out):
@@ -58,10 +59,14 @@ def tile_salad_pa_l_kernel(tc, x, Ws1, bs1, Ws2, out):
         w2s = const.tile([P, 2, KP2 * P], U8, name="w2s", align_bytes=64)
         accs = []
         for k in range(NACC):
-            acc = const.tile([P, M + 1], F32, name="acc%d" % k)
-            nc.vector.memset(acc[:], 0.0)
+            acc = const.tile([P, M], F32, name="acc%d" % k)
             accs.append(acc)
-        junk = const.tile([P, M], F32, name="junk")
+        dust = const.tile([P, M + 1], F32, name="dust")
+        nc.vector.memset(dust[:], 0.0)
+        junks = []
+        for k in range(NACC):
+            junk = const.tile([P, M], BF16, name="junk%d" % k)
+            junks.append(junk)
         junk32 = const.tile([P, NT], F32, name="junk32")
 
         xraw = {}
@@ -78,10 +83,10 @@ def tile_salad_pa_l_kernel(tc, x, Ws1, bs1, Ws2, out):
                 )
                 xraw[(q, g)] = t
 
-        def inter(q, g, share):
+        def inter(q, g, on_scalar):
             src = xraw.pop((q, g))
             t = xgp.tile([P, NCH, 4], BF16, name="xgrp", tag="xgrp", align_bytes=64)
-            if g in share:
+            if on_scalar:
                 nc.scalar.copy(out=t[:], in_=src[:].rearrange("p j n -> p n j"))
             else:
                 nc.vector.tensor_copy(out=t[:], in_=src[:].rearrange("p j n -> p n j"))
@@ -146,12 +151,20 @@ def tile_salad_pa_l_kernel(tc, x, Ws1, bs1, Ws2, out):
             nc.vector.quantize_mx(out=cod[:].bitcast(FP8X4), scales=sca[:], in_=grp[:].rearrange("p n j -> p (n j)"))
             hscod[(q, g)] = (cod, sca)
 
-        def stage1(q, share, woven):
+        def on_scalar(q, j):
+            if q < CPI:
+                return j % 2 == 1
+            slot = 8 * (q % CPI) + j
+            return PHASES[1][0] <= slot < PHASES[1][1] and slot not in V_IN_SWEEPS
+
+        def stage1(q, woven, late):
             raw = None
             for j in range(8):
                 g2, t = divmod(j, 4)
+                if j == LAG and late:
+                    late.pop(0)()
                 if q + 1 < NQ and j < KP1:
-                    inter(q + 1, j, share)
+                    inter(q + 1, j, on_scalar(q, j))
                 if q + 1 < NQ and 1 <= j <= KP1:
                     quant(q + 1, j - 1)
                 if pend and t == 1:
@@ -175,7 +188,7 @@ def tile_salad_pa_l_kernel(tc, x, Ws1, bs1, Ws2, out):
                     grp = hsp.tile([P, NCH, 4], BF16, name="hgrp", tag="hgrp", bufs=2, align_bytes=64)
                     nc.vector.tensor_copy(out=grp[:], in_=raw[:].rearrange("p j n -> p n j"))
                     pend.append((q, g2, grp))
-                for step in woven.pop((q % CPI) * 8 + j, ()):
+                for step in woven.pop(8 * q + j, ()):
                     step()
             for g in range(KP1):
                 xcod.pop((q, g))
@@ -208,6 +221,8 @@ def tile_salad_pa_l_kernel(tc, x, Ws1, bs1, Ws2, out):
 
         def sinkhorn_steps(b, pt, mx, last):
             s = {}
+            row_pe = TAIL_ROW_PE if last else 0
+            col_pe = TAIL_COL_PE if last else 0
 
             def shift():
                 m2 = small.tile([P, 2], F32, name="m2", tag="m2")
@@ -216,7 +231,6 @@ def tile_salad_pa_l_kernel(tc, x, Ws1, bs1, Ws2, out):
                 nc.vector.tensor_scalar(out=negm[:], in0=m2[:], scalar1=-1.0, scalar2=None, op0=ALU.mult)
                 s["negm"] = negm
                 s["r1"] = small.tile([P, 2 * CPI], F32, name="r1", tag="r1")
-                s["et"] = etp.tile([P, NT, M], F32, name="et", tag="et")
 
             def exps(c):
                 for h in range(2):
@@ -226,6 +240,8 @@ def tile_salad_pa_l_kernel(tc, x, Ws1, bs1, Ws2, out):
                     )
 
             def turn(c):
+                if c == 0:
+                    s["et"] = etp.tile([P, NT, M], F32, name="et", tag="et")
                 et = s["et"]
                 banks = []
                 for half in range(2):
@@ -255,19 +271,41 @@ def tile_salad_pa_l_kernel(tc, x, Ws1, bs1, Ws2, out):
                 nc.vector.reciprocal(out=abc[:, 0:M], in_=rb[:, 0:M])
                 nc.vector.memset(abc[:, M : M + 1], 1.0)
                 s["abc"] = abc
+                if col_pe:
+                    acol = small.tile([P, 2], F32, name="acol", tag="acol")
+                    nc.vector.reciprocal(out=acol[:], in_=rc[:])
+                    s["acol"] = acol
+
+            def col_tensor():
+                cp = pstr.tile([P, NCH], F32, name="cp", tag="tr")
+                for t in range(NT - col_pe, NT):
+                    for h in range(2):
+                        lo = P * (t % 4)
+                        nc.tensor.matmul(
+                            cp[:, t : t + 1], lhsT=pt[(h, t // 4)][:, lo : lo + P], rhs=s["acol"][:, h : h + 1],
+                            start=(h == 0), stop=(h == 1),
+                        )
+                s["cp"] = cp
 
             def col_part(t0):
                 if t0 == 0:
                     s["cc"] = small.tile([P, NT], F32, name="cc", tag="cc")
-                for t in range(t0, t0 + 4):
+                for t in range(t0, min(t0 + 4, NT - col_pe)):
                     nc.vector.scalar_tensor_tensor(
-                        out=junk[:], in0=s["et"][:, t, :], scalar=1.0, in1=s["abc"][:, 0:M], op0=ALU.mult, op1=ALU.mult,
+                        out=junks[t % NACC][:], in0=s["et"][:, t, :], scalar=1.0, in1=s["abc"][:, 0:M], op0=ALU.mult, op1=ALU.mult,
                         accum_out=s["cc"][:, t : t + 1],
                     )
 
             def col_end():
                 cd = small.tile([P, NT], F32, name="cd", tag="cd")
-                nc.vector.tensor_scalar(out=cd[:], in0=s["cc"][:], scalar1=s["abc"][:, M : M + 1], scalar2=None, op0=ALU.add)
+                nv = NT - col_pe
+                nc.vector.tensor_scalar(
+                    out=cd[:, 0:nv], in0=s["cc"][:, 0:nv], scalar1=s["abc"][:, M : M + 1], scalar2=None, op0=ALU.add
+                )
+                if col_pe:
+                    nc.vector.tensor_scalar(
+                        out=cd[:, nv:NT], in0=s["cp"][:, nv:NT], scalar1=s["abc"][:, M : M + 1], scalar2=None, op0=ALU.add
+                    )
                 bb = small.tile([P, NT], F32, name="bb", tag="bb")
                 nc.vector.reciprocal(out=bb[:], in_=cd[:])
                 s["bb"] = bb
@@ -277,26 +315,29 @@ def tile_salad_pa_l_kernel(tc, x, Ws1, bs1, Ws2, out):
                 if t0 == 0:
                     nc.vector.tensor_scalar(
                         out=junk32[:], in0=bb[:], scalar1=1.0 / NPIX, scalar2=None, op0=ALU.mult, op1=ALU.add,
-                        accum_out=accs[0][:, M : M + 1],
+                        accum_out=dust[:, M : M + 1],
                     )
-                for t in range(t0, t0 + 4):
+                for t in range(t0, min(t0 + 4, NT - row_pe)):
                     acc = accs[t % NACC]
                     if t < NACC:
                         nc.vector.tensor_scalar(
-                            out=acc[:, 0:M], in0=et[:, t, :], scalar1=bb[:, t : t + 1], scalar2=None, op0=ALU.mult
+                            out=acc[:], in0=et[:, t, :], scalar1=bb[:, t : t + 1], scalar2=None, op0=ALU.mult
                         )
                     else:
                         nc.vector.scalar_tensor_tensor(
-                            out=acc[:, 0:M], in0=et[:, t, :], scalar=bb[:, t : t + 1], in1=acc[:, 0:M],
-                            op0=ALU.mult, op1=ALU.add,
+                            out=acc[:], in0=et[:, t, :], scalar=bb[:, t : t + 1], in1=acc[:], op0=ALU.mult, op1=ALU.add
                         )
 
             def row_end():
+                et, bb = s["et"], s["bb"]
                 rb = pstr.tile([P, NCH], F32, name="rb", tag="tr")
-                for k in range(NACC):
+                nc.tensor.matmul(rb[:, 0 : M + 1], lhsT=ones[:], rhs=dust[:], start=True, stop=False)
+                for t in range(NT - row_pe, NT):
                     nc.tensor.matmul(
-                        rb[:, 0 : M + 1], lhsT=ones[:], rhs=accs[k][:], start=(k == 0), stop=(k == NACC - 1)
+                        rb[:, 0:M], lhsT=bb[:, t : t + 1].to_broadcast([P, P]), rhs=et[:, t, :], start=False, stop=False
                     )
+                for k in range(NACC):
+                    nc.tensor.matmul(rb[:, 0:M], lhsT=ones[:], rhs=accs[k][:], start=False, stop=(k == NACC - 1))
                 abc = small.tile([P, M + 1], F32, name="abc", tag="abc")
                 nc.vector.reciprocal(out=abc[:], in_=rb[:, 0 : M + 1])
                 s["abc"] = abc
@@ -336,7 +377,7 @@ def tile_salad_pa_l_kernel(tc, x, Ws1, bs1, Ws2, out):
                     nc.scalar.activation(
                         out=osb[:], in_=banks[h][:].rearrange("p t n -> p (t n)"), func=ACT.Copy, scale=s["acol"][:, h : h + 1]
                     )
-                    nc.gpsimd.dma_start(out=out[b, P * h : P * (h + 1), NCH * c : NCH * (c + 1)], in_=osb[:])
+                    nc.sync.dma_start(out=out[b, P * h : P * (h + 1), NCH * c : NCH * (c + 1)], in_=osb[:])
 
             def bind(f, arg):
                 return lambda: f(arg)
@@ -349,48 +390,63 @@ def tile_salad_pa_l_kernel(tc, x, Ws1, bs1, Ws2, out):
             prep.append(bind(turn, CPI - 1))
             sweeps = []
             for it in range(3):
-                for t0 in range(0, NT, 4):
+                if col_pe:
+                    sweeps.append(col_tensor)
+                for t0 in range(0, NT - col_pe, 4):
                     sweeps.append(bind(col_part, t0))
                 sweeps.append(col_end)
                 if it < 2:
-                    for t0 in range(0, NT, 4):
+                    for t0 in range(0, NT - row_pe, 4):
                         sweeps.append(bind(row_part, t0))
                     sweeps.append(row_end)
-            fin = [a_column, bind(scale_b, 0)]
+                    if col_pe or it == 1:
+                        sweeps.append(a_column)
+            fin = [bind(scale_b, 0)]
             for c in range(1, CPI):
                 fin.append(bind(scale_b, c))
                 fin.append(bind(store, c - 1))
             fin.append(bind(store, CPI - 1))
             return (prep, sweeps, fin)
 
-        def weave(lists):
-            woven = {}
+        def weave(lists, first, woven):
             for steps, (lo, hi) in zip(lists, PHASES):
                 for i, step in enumerate(steps):
-                    slot = lo + (i * (hi - lo)) // len(steps)
+                    slot = first + lo + (i * (hi - lo)) // len(steps)
                     woven[slot] = woven.get(slot, []) + [step]
-            return woven
 
         load(1)
         for g in range(KP1):
-            inter(0, g, S_IDLE)
+            inter(0, g, g % 2 == 1)
             quant(0, g)
         woven = {}
-        pt, mx = {}, None
-        for q in range(NQ):
+        late = []
+        state = {}
+
+        def second(q):
             b, c = divmod(q, CPI)
             if c == 0:
-                pt = {}
-                mx = small.tile([P, 2 * CPI], F32, name="mx", tag="mx")
-            if q + 2 < NQ:
-                load(q + 2)
-            stage1(q, S_BUSY[c] if b > 0 else S_IDLE, woven)
-            stage2(q, pt, mx)
+                state["pt"] = {}
+                state["mx"] = small.tile([P, 2 * CPI], F32, name="mx", tag="mx")
+            stage2(q, state["pt"], state["mx"])
             if c == CPI - 1:
-                lists = sinkhorn_steps(b, pt, mx, b == B - 1)
+                lists = sinkhorn_steps(b, state["pt"], state["mx"], b == B - 1)
                 if b < B - 1:
-                    woven = weave(lists)
+                    weave(lists, 8 * (q + 1), woven)
                 else:
                     for steps in lists:
                         for step in steps:
                             step()
+
+        def bind_second(q):
+            return lambda: second(q)
+
+        for q in range(NQ):
+            b, c = divmod(q, CPI)
+            if q + 2 < NQ:
+                load(q + 2)
+            stage1(q, woven, late)
+            late.append(bind_second(q))
+        for slot in sorted(woven):
+            for step in woven[slot]:
+                step()
+        late.pop(0)()

@@ -86,10 +86,12 @@ def tile_salad_pa_l_kernel(tc, x, Ws1, bs1, Ws2, out):
         def inter(q, g, on_scalar):
             src = xraw.pop((q, g))
             t = xgp.tile([P, NCH, 4], BF16, name="xgrp", tag="xgrp", align_bytes=64)
+            dst4 = t[:].rearrange("p (c i) j -> p c j i", i=4)
+            src4 = src[:].rearrange("p j (c i) -> p c j i", i=4)
             if on_scalar:
-                nc.scalar.copy(out=t[:], in_=src[:].rearrange("p j n -> p n j"))
+                nc.scalar.copy(out=dst4, in_=src4)
             else:
-                nc.vector.tensor_copy(out=t[:], in_=src[:].rearrange("p j n -> p n j"))
+                nc.vector.tensor_copy(out=dst4, in_=src4)
             xgrp[(q, g)] = t
 
         def quant(q, g):
@@ -186,7 +188,9 @@ def tile_salad_pa_l_kernel(tc, x, Ws1, bs1, Ws2, out):
                 nc.scalar.activation(out=raw[:, t, :], in_=acc[:], func=ACT.Relu, bias=b1[:, g2, t : t + 1], scale=1.0)
                 if t == 3:
                     grp = hsp.tile([P, NCH, 4], BF16, name="hgrp", tag="hgrp", bufs=2, align_bytes=64)
-                    nc.vector.tensor_copy(out=grp[:], in_=raw[:].rearrange("p j n -> p n j"))
+                    nc.vector.tensor_copy(
+                        out=grp[:].rearrange("p (c i) j -> p c j i", i=4), in_=raw[:].rearrange("p j (c i) -> p c j i", i=4)
+                    )
                     pend.append((q, g2, grp))
                 for step in woven.pop(8 * q + j, ()):
                     step()

@@ -23,9 +23,14 @@ KP1 = C // 512
 KP2 = HID // 512
 NT = NPIX // P
 NACC = 4
+NJUNK = 4
 LAG = 3
 PHASES = ((4, 13), (13, 59), (59, 68))
 V_IN_SWEEPS = (29, 45, 53)
+ET_V = 2
+XT_V = 99
+XT_G = False
+OUT_V = 99
 TAIL_ROW_PE = 0
 TAIL_COL_PE = 0
 
@@ -36,7 +41,7 @@ def tile_salad_pa_l_kernel(tc, x, Ws1, bs1, Ws2, out):
 
     with ExitStack() as ctx:
         const = ctx.enter_context(tc.tile_pool(name="const", bufs=1))
-        xrp = ctx.enter_context(tc.tile_pool(name="xrp", bufs=8))
+        xrp = ctx.enter_context(tc.tile_pool(name="xrp", bufs=16))
         xgp = ctx.enter_context(tc.tile_pool(name="xgp", bufs=3))
         xcp = ctx.enter_context(tc.tile_pool(name="xcp", bufs=12))
         hsp = ctx.enter_context(tc.tile_pool(name="hsp", bufs=2))
@@ -59,12 +64,11 @@ def tile_salad_pa_l_kernel(tc, x, Ws1, bs1, Ws2, out):
         w2s = const.tile([P, 2, KP2 * P], U8, name="w2s", align_bytes=64)
         accs = []
         for k in range(NACC):
-            acc = const.tile([P, M], F32, name="acc%d" % k)
+            acc = const.tile([P, M + 1], F32, name="acc%d" % k)
+            nc.vector.memset(acc[:], 0.0)
             accs.append(acc)
-        dust = const.tile([P, M + 1], F32, name="dust")
-        nc.vector.memset(dust[:], 0.0)
         junks = []
-        for k in range(NACC):
+        for k in range(NJUNK):
             junk = const.tile([P, M], BF16, name="junk%d" % k)
             junks.append(junk)
         junk32 = const.tile([P, NT], F32, name="junk32")
@@ -76,7 +80,7 @@ def tile_salad_pa_l_kernel(tc, x, Ws1, bs1, Ws2, out):
         def load(q):
             b, c = divmod(q, CPI)
             for g in range(KP1):
-                t = xrp.tile([P, 4, NCH], BF16, name="xraw", tag="xraw")
+                t = xrp.tile([P, 4, NCH], BF16, name="xraw", tag="k4")
                 nc.sync.dma_start(
                     out=t[:],
                     in_=xv[b, 512 * g : 512 * (g + 1), NCH * c : NCH * (c + 1)].rearrange("(p j) n -> p j n", j=4),
@@ -103,7 +107,7 @@ def tile_salad_pa_l_kernel(tc, x, Ws1, bs1, Ws2, out):
 
         def turn_weights(head, rows, passes, cod, sca, eng0):
             words = rows[:].bitcast(F32)
-            grp = head.tile([P, KP1, P, 4], BF16, name="wgrp", tag="wgrp", bufs=2, align_bytes=64)
+            grp = head.tile([P, KP1, P, 4], BF16, name="wgrp", tag="wgrp", bufs=1, align_bytes=64)
             gw = grp[:].bitcast(F32)
             for gp in range(passes // 2):
                 bank = pstr.tile([P, 2, 2, P], F32, name="wbank", tag="tr")
@@ -127,19 +131,28 @@ def tile_salad_pa_l_kernel(tc, x, Ws1, bs1, Ws2, out):
 
         w1v = Ws1.rearrange("(g m t) k -> g t m k", g=2, t=4)
         with tc.tile_pool(name="head", bufs=2) as head:
+            wrows = []
             for j in range(8):
-                rows = head.tile([P, C], BF16, name="wrow", tag="wrow", bufs=3)
+                rows = head.tile([P, C], BF16, name="wrow", tag="wrow", bufs=8)
                 nc.sync.dma_start(out=rows[:], in_=w1v[j // 4, j % 4])
-                turn_weights(head, rows, KP1, w1c[:, j, :], w1s[:, j, :], j)
-                if j == 1:
+                wrows.append(rows)
+                if j == 0:
                     load(0)
             for h in range(2):
                 rows2 = head.tile([P, HID], BF16, name="wrow2", tag="wrow2", bufs=2)
                 nc.sync.dma_start(out=rows2[:], in_=Ws2[P * h : P * (h + 1), :])
-                turn_weights(head, rows2, KP2, w2c[:, h, :], w2s[:, h, :], h)
+                wrows.append(rows2)
+            load(1)
+            for j in range(8):
+                turn_weights(head, wrows[j], KP1, w1c[:, j, :], w1s[:, j, :], j)
+                if j == 0:
+                    for g in range(KP1):
+                        inter(0, g, g % 2 == 1)
+                        quant(0, g)
+            for h in range(2):
+                turn_weights(head, wrows[8 + h], KP2, w2c[:, h, :], w2s[:, h, :], h)
 
         pp = ctx.enter_context(tc.tile_pool(name="pp", bufs=20))
-        etp = ctx.enter_context(tc.tile_pool(name="etp", bufs=1))
         xtp = ctx.enter_context(tc.tile_pool(name="xtp", bufs=8))
         outp = ctx.enter_context(tc.tile_pool(name="outp", bufs=3))
 
@@ -244,9 +257,8 @@ def tile_salad_pa_l_kernel(tc, x, Ws1, bs1, Ws2, out):
                     )
 
             def turn(c):
-                if c == 0:
-                    s["et"] = etp.tile([P, NT, M], F32, name="et", tag="et")
-                et = s["et"]
+                et = xrp.tile([P, 4, M], F32, name="et", tag="k4")
+                s[("et", c)] = et
                 banks = []
                 for half in range(2):
                     bank = pstr.tile([P, 2, 2, P], F32, name="ebank", tag="tr")
@@ -256,8 +268,8 @@ def tile_salad_pa_l_kernel(tc, x, Ws1, bs1, Ws2, out):
                             nc.tensor.transpose(bank[:, tt, h, :], pt[(h, c)][:, lo : lo + P], ident[:])
                     banks.append(bank)
                 for half in range(2):
-                    t0 = 4 * c + 2 * half
-                    if last and half == 0:
+                    t0 = 2 * half
+                    if last or (half == 0 and c % ET_V == 0):
                         nc.vector.tensor_copy(out=et[:, t0 : t0 + 2, :], in_=banks[half][:].rearrange("p t h i -> p t (h i)"))
                     else:
                         nc.scalar.copy(out=et[:, t0 : t0 + 2, :], in_=banks[half][:].rearrange("p t h i -> p t (h i)"))
@@ -296,7 +308,7 @@ def tile_salad_pa_l_kernel(tc, x, Ws1, bs1, Ws2, out):
                     s["cc"] = small.tile([P, NT], F32, name="cc", tag="cc")
                 for t in range(t0, min(t0 + 4, NT - col_pe)):
                     nc.vector.scalar_tensor_tensor(
-                        out=junks[t % NACC][:], in0=s["et"][:, t, :], scalar=1.0, in1=s["abc"][:, 0:M], op0=ALU.mult, op1=ALU.mult,
+                        out=junks[t % NJUNK][:], in0=s[("et", t // 4)][:, t % 4, :], scalar=1.0, in1=s["abc"][:, 0:M], op0=ALU.mult, op1=ALU.mult,
                         accum_out=s["cc"][:, t : t + 1],
                     )
 
@@ -314,34 +326,39 @@ def tile_salad_pa_l_kernel(tc, x, Ws1, bs1, Ws2, out):
                 nc.vector.reciprocal(out=bb[:], in_=cd[:])
                 s["bb"] = bb
 
+            def col_end_part(c):
+                if c == 0:
+                    s["cd"] = small.tile([P, NT], F32, name="cd", tag="cd")
+                    s["bb"] = small.tile([P, NT], F32, name="bb", tag="bb")
+                nc.vector.tensor_scalar(
+                    out=s["cd"][:, 4 * c : 4 * c + 4], in0=s["cc"][:, 4 * c : 4 * c + 4], scalar1=s["abc"][:, M : M + 1],
+                    scalar2=None, op0=ALU.add,
+                )
+                nc.vector.reciprocal(out=s["bb"][:, 4 * c : 4 * c + 4], in_=s["cd"][:, 4 * c : 4 * c + 4])
+
             def row_part(t0):
-                et, bb = s["et"], s["bb"]
+                et, bb = s[("et", t0 // 4)], s["bb"]
                 if t0 == 0:
                     nc.vector.tensor_scalar(
                         out=junk32[:], in0=bb[:], scalar1=1.0 / NPIX, scalar2=None, op0=ALU.mult, op1=ALU.add,
-                        accum_out=dust[:, M : M + 1],
+                        accum_out=accs[0][:, M : M + 1],
                     )
                 for t in range(t0, min(t0 + 4, NT - row_pe)):
                     acc = accs[t % NACC]
                     if t < NACC:
                         nc.vector.tensor_scalar(
-                            out=acc[:], in0=et[:, t, :], scalar1=bb[:, t : t + 1], scalar2=None, op0=ALU.mult
+                            out=acc[:, 0:M], in0=et[:, t % 4, :], scalar1=bb[:, t : t + 1], scalar2=None, op0=ALU.mult
                         )
                     else:
                         nc.vector.scalar_tensor_tensor(
-                            out=acc[:], in0=et[:, t, :], scalar=bb[:, t : t + 1], in1=acc[:], op0=ALU.mult, op1=ALU.add
+                            out=acc[:, 0:M], in0=et[:, t % 4, :], scalar=bb[:, t : t + 1], in1=acc[:, 0:M],
+                            op0=ALU.mult, op1=ALU.add,
                         )
 
             def row_end():
-                et, bb = s["et"], s["bb"]
                 rb = pstr.tile([P, NCH], F32, name="rb", tag="tr")
-                nc.tensor.matmul(rb[:, 0 : M + 1], lhsT=ones[:], rhs=dust[:], start=True, stop=False)
-                for t in range(NT - row_pe, NT):
-                    nc.tensor.matmul(
-                        rb[:, 0:M], lhsT=bb[:, t : t + 1].to_broadcast([P, P]), rhs=et[:, t, :], start=False, stop=False
-                    )
                 for k in range(NACC):
-                    nc.tensor.matmul(rb[:, 0:M], lhsT=ones[:], rhs=accs[k][:], start=False, stop=(k == NACC - 1))
+                    nc.tensor.matmul(rb[:, 0 : M + 1], lhsT=ones[:], rhs=accs[k][:], start=(k == 0), stop=(k == NACC - 1))
                 abc = small.tile([P, M + 1], F32, name="abc", tag="abc")
                 nc.vector.reciprocal(out=abc[:], in_=rb[:, 0 : M + 1])
                 s["abc"] = abc
@@ -359,12 +376,17 @@ def tile_salad_pa_l_kernel(tc, x, Ws1, bs1, Ws2, out):
                 xts = []
                 for t in range(4 * c, 4 * c + 4):
                     xt = xtp.tile([P, M], F32, name="xt", tag="xt")
-                    if last:
+                    if t % XT_V == 0:
                         nc.vector.tensor_scalar(
-                            out=xt[:], in0=s["et"][:, t, :], scalar1=s["bb"][:, t : t + 1], scalar2=None, op0=ALU.mult
+                            out=xt[:], in0=s[("et", c)][:, t % 4, :], scalar1=s["bb"][:, t : t + 1], scalar2=None, op0=ALU.mult
+                        )
+                    elif XT_G:
+                        nc.gpsimd.tensor_scalar(
+                            out=xt[:], in0=s[("et", c)][:, t % 4, :], scalar1=s["bb"][:, t : t + 1], scalar2=0.0,
+                            op0=ALU.mult, op1=ALU.add,
                         )
                     else:
-                        nc.scalar.activation(out=xt[:], in_=s["et"][:, t, :], func=ACT.Copy, scale=s["bb"][:, t : t + 1])
+                        nc.scalar.activation(out=xt[:], in_=s[("et", c)][:, t % 4, :], func=ACT.Copy, scale=s["bb"][:, t : t + 1])
                     xts.append(xt)
                 s[("xt", c)] = xts
 
@@ -372,15 +394,27 @@ def tile_salad_pa_l_kernel(tc, x, Ws1, bs1, Ws2, out):
                 xts = s.pop(("xt", c))
                 banks = []
                 for h in range(2):
-                    ob = pstr.tile([P, 4, P], F32, name="ob", tag="tr")
+                    if last:
+                        ob = ps1.tile([P, 4, P], F32, name="ob1", tag="s1")
+                    else:
+                        ob = pstr.tile([P, 4, P], F32, name="ob", tag="tr")
                     for tt in range(4):
                         nc.tensor.transpose(ob[:, tt, :], xts[tt][:, P * h : P * (h + 1)], ident[:])
                     banks.append(ob)
                 for h in range(2):
-                    osb = outp.tile([P, NCH], F32, name="osb", tag="osb")
-                    nc.scalar.activation(
-                        out=osb[:], in_=banks[h][:].rearrange("p t n -> p (t n)"), func=ACT.Copy, scale=s["acol"][:, h : h + 1]
-                    )
+                    if last:
+                        osb = xrp.tile([P, NCH], F32, name="osbl", tag="k4")
+                    else:
+                        osb = outp.tile([P, NCH], F32, name="osb", tag="osb")
+                    if h == 0 and c % (2 if last else OUT_V) == 0:
+                        nc.vector.tensor_scalar(
+                            out=osb[:], in0=banks[h][:].rearrange("p t n -> p (t n)"), scalar1=s["acol"][:, h : h + 1],
+                            scalar2=None, op0=ALU.mult,
+                        )
+                    else:
+                        nc.scalar.activation(
+                            out=osb[:], in_=banks[h][:].rearrange("p t n -> p (t n)"), func=ACT.Copy, scale=s["acol"][:, h : h + 1]
+                        )
                     nc.sync.dma_start(out=out[b, P * h : P * (h + 1), NCH * c : NCH * (c + 1)], in_=osb[:])
 
             def bind(f, arg):
@@ -410,6 +444,16 @@ def tile_salad_pa_l_kernel(tc, x, Ws1, bs1, Ws2, out):
                 fin.append(bind(scale_b, c))
                 fin.append(bind(store, c - 1))
             fin.append(bind(store, CPI - 1))
+            if last:
+                sweeps = sweeps[0 : len(sweeps) - CPI - 1]
+                fin = []
+                for c in range(CPI + 2):
+                    if c < CPI:
+                        fin.extend([bind(col_part, 4 * c), bind(col_end_part, c)])
+                    if 1 <= c <= CPI:
+                        fin.append(bind(scale_b, c - 1))
+                    if c >= 2:
+                        fin.append(bind(store, c - 2))
             return (prep, sweeps, fin)
 
         def weave(lists, first, woven):
@@ -418,10 +462,6 @@ def tile_salad_pa_l_kernel(tc, x, Ws1, bs1, Ws2, out):
                     slot = first + lo + (i * (hi - lo)) // len(steps)
                     woven[slot] = woven.get(slot, []) + [step]
 
-        load(1)
-        for g in range(KP1):
-            inter(0, g, g % 2 == 1)
-            quant(0, g)
         woven = {}
         late = []
         state = {}
@@ -434,10 +474,17 @@ def tile_salad_pa_l_kernel(tc, x, Ws1, bs1, Ws2, out):
             stage2(q, state["pt"], state["mx"])
             if c == CPI - 1:
                 lists = sinkhorn_steps(b, state["pt"], state["mx"], b == B - 1)
-                if b < B - 1:
+                if b < B - 2:
                     weave(lists, 8 * (q + 1), woven)
+                elif b == B - 2:
+                    weave(lists[0:2], 8 * (q + 1), woven)
+                    state["held"] = lists[2]
                 else:
-                    for steps in lists:
+                    for step in lists[0]:
+                        step()
+                    for step in state["held"]:
+                        step()
+                    for steps in lists[1:]:
                         for step in steps:
                             step()
 

@@ -16,23 +16,21 @@ ACT = mybir.ActivationFunctionType
 AX = mybir.AxisListType
 
 P = 128
+K_PASS = 512
 NCH = 512
 CPI = NPIX // NCH
 NQ = B * CPI
-KP1 = C // 512
-KP2 = HID // 512
+KP1 = C // K_PASS
+KP2 = HID // K_PASS
+TILES1 = HID // P
+MH = M // P
 NT = NPIX // P
+TPC = NCH // P
 NACC = 4
 NJUNK = 4
 LAG = 3
 PHASES = ((4, 13), (13, 59), (59, 68))
 V_IN_SWEEPS = (29, 45, 53)
-ET_V = 2
-XT_V = 99
-XT_G = False
-OUT_V = 99
-TAIL_ROW_PE = 0
-TAIL_COL_PE = 0
 
 
 def tile_salad_pa_l_kernel(tc, x, Ws1, bs1, Ws2, out):
@@ -43,11 +41,11 @@ def tile_salad_pa_l_kernel(tc, x, Ws1, bs1, Ws2, out):
         const = ctx.enter_context(tc.tile_pool(name="const", bufs=1))
         xrp = ctx.enter_context(tc.tile_pool(name="xrp", bufs=16))
         xgp = ctx.enter_context(tc.tile_pool(name="xgp", bufs=3))
-        xcp = ctx.enter_context(tc.tile_pool(name="xcp", bufs=12))
+        xcp = ctx.enter_context(tc.tile_pool(name="xcp", bufs=2 * KP1))
         hsp = ctx.enter_context(tc.tile_pool(name="hsp", bufs=2))
         small = ctx.enter_context(tc.tile_pool(name="small", bufs=2))
         ps1 = ctx.enter_context(tc.psum_pool(name="ps1", bufs=4))
-        ps2 = ctx.enter_context(tc.psum_pool(name="ps2", bufs=2))
+        ps2 = ctx.enter_context(tc.psum_pool(name="ps2", bufs=MH))
         pstr = ctx.enter_context(tc.psum_pool(name="pstr", bufs=2))
 
         ident = const.tile([P, P], F32, name="ident")
@@ -56,405 +54,380 @@ def tile_salad_pa_l_kernel(tc, x, Ws1, bs1, Ws2, out):
         nc.vector.memset(ones[:], 1.0)
         warm = const.tile([P, 1], F32, name="warm")
         nc.scalar.activation(out=warm[:], in_=ones[:, 0:1], func=ACT.Exp)
-        b1 = const.tile([P, 2, 4], BF16, name="b1")
-        nc.sync.dma_start(out=b1[:], in_=bs1.rearrange("(g p t) -> p g t", g=2, t=4))
-        w1c = const.tile([P, 8, KP1 * P], U32, name="w1c", align_bytes=64)
-        w1s = const.tile([P, 8, KP1 * P], U8, name="w1s", align_bytes=64)
-        w2c = const.tile([P, 2, KP2 * P], U32, name="w2c", align_bytes=64)
-        w2s = const.tile([P, 2, KP2 * P], U8, name="w2s", align_bytes=64)
+        bias = const.tile([P, KP2, 4], BF16, name="bias")
+        nc.sync.dma_start(out=bias[:], in_=bs1.rearrange("(g p t) -> p g t", g=KP2, t=4))
+        w1c = const.tile([P, TILES1, KP1 * P], U32, name="w1c", align_bytes=64)
+        w1s = const.tile([P, TILES1, KP1 * P], U8, name="w1s", align_bytes=64)
+        w2c = const.tile([P, MH, KP2 * P], U32, name="w2c", align_bytes=64)
+        w2s = const.tile([P, MH, KP2 * P], U8, name="w2s", align_bytes=64)
         accs = []
-        for k in range(NACC):
-            acc = const.tile([P, M + 1], F32, name="acc%d" % k)
+        for idx in range(NACC):
+            acc = const.tile([P, M + 1], F32, name="acc%d" % idx)
             nc.vector.memset(acc[:], 0.0)
             accs.append(acc)
         junks = []
-        for k in range(NJUNK):
-            junk = const.tile([P, M], BF16, name="junk%d" % k)
+        for idx in range(NJUNK):
+            junk = const.tile([P, M], BF16, name="junk%d" % idx)
             junks.append(junk)
-        junk32 = const.tile([P, NT], F32, name="junk32")
+        junk_b = const.tile([P, NT], F32, name="junk_b")
 
-        xraw = {}
-        xgrp = {}
-        xcod = {}
+        def interleaved(grouped, rows):
+            return (
+                grouped[:].rearrange("p (c i) j -> p c j i", i=4),
+                rows[:].rearrange("p j (c i) -> p c j i", i=4),
+            )
 
-        def load(q):
-            b, c = divmod(q, CPI)
+        x_rows = {}
+        x_grouped = {}
+        x_codes = {}
+
+        def load_chunk(q):
+            img, c = divmod(q, CPI)
             for g in range(KP1):
-                t = xrp.tile([P, 4, NCH], BF16, name="xraw", tag="k4")
+                x_tile = xrp.tile([P, 4, NCH], BF16, name="x_rows", tag="x_or_et")
                 nc.sync.dma_start(
-                    out=t[:],
-                    in_=xv[b, 512 * g : 512 * (g + 1), NCH * c : NCH * (c + 1)].rearrange("(p j) n -> p j n", j=4),
+                    out=x_tile[:],
+                    in_=xv[img, K_PASS * g : K_PASS * (g + 1), NCH * c : NCH * (c + 1)].rearrange("(p j) n -> p j n", j=4),
                 )
-                xraw[(q, g)] = t
+                x_rows[(q, g)] = x_tile
 
-        def inter(q, g, on_scalar):
-            src = xraw.pop((q, g))
-            t = xgp.tile([P, NCH, 4], BF16, name="xgrp", tag="xgrp", align_bytes=64)
-            dst4 = t[:].rearrange("p (c i) j -> p c j i", i=4)
-            src4 = src[:].rearrange("p j (c i) -> p c j i", i=4)
+        def interleave_x(q, g, on_scalar):
+            grouped = xgp.tile([P, NCH, 4], BF16, name="x_grouped", tag="x_grouped", align_bytes=64)
+            dst, src = interleaved(grouped, x_rows.pop((q, g)))
             if on_scalar:
-                nc.scalar.copy(out=dst4, in_=src4)
+                nc.scalar.copy(out=dst, in_=src)
             else:
-                nc.vector.tensor_copy(out=dst4, in_=src4)
-            xgrp[(q, g)] = t
+                nc.vector.tensor_copy(out=dst, in_=src)
+            x_grouped[(q, g)] = grouped
 
-        def quant(q, g):
-            src = xgrp.pop((q, g))
-            cod = xcp.tile([P, NCH], U32, name="xcod", tag="xcod", align_bytes=64)
-            sca = xcp.tile([P, NCH], U8, name="xsca", tag="xsca", align_bytes=64)
-            nc.vector.quantize_mx(out=cod[:].bitcast(FP8X4), scales=sca[:], in_=src[:].rearrange("p n j -> p (n j)"))
-            xcod[(q, g)] = (cod, sca)
+        def quantize_x(q, g):
+            grouped = x_grouped.pop((q, g))
+            codes = xcp.tile([P, NCH], U32, name="x_codes", tag="x_codes", align_bytes=64)
+            scales = xcp.tile([P, NCH], U8, name="x_scales", tag="x_scales", align_bytes=64)
+            nc.vector.quantize_mx(
+                out=codes[:].bitcast(FP8X4), scales=scales[:], in_=grouped[:].rearrange("p n j -> p (n j)")
+            )
+            x_codes[(q, g)] = (codes, scales)
 
-        def turn_weights(head, rows, passes, cod, sca, eng0):
-            words = rows[:].bitcast(F32)
-            grp = head.tile([P, KP1, P, 4], BF16, name="wgrp", tag="wgrp", bufs=1, align_bytes=64)
-            gw = grp[:].bitcast(F32)
-            for gp in range(passes // 2):
-                bank = pstr.tile([P, 2, 2, P], F32, name="wbank", tag="tr")
-                for g2 in range(2):
-                    g = 2 * gp + g2
+        def quantize_weights(head, w_tile, passes, codes, scales, first_engine):
+            words = w_tile[:].bitcast(F32)
+            grouped = head.tile([P, KP1, P, 4], BF16, name="w_grouped", tag="w_grouped", bufs=1, align_bytes=64)
+            grouped_words = grouped[:].bitcast(F32)
+            for pair in range(passes // 2):
+                bank = pstr.tile([P, 2, 2, P], F32, name="w_turned", tag="turned")
+                for which in range(2):
+                    g = 2 * pair + which
                     for u in range(2):
-                        nc.tensor.transpose(bank[:, g2, u, :], words[:, 256 * g + u : 256 * (g + 1) : 2], ident[:])
-                if (gp + eng0) % 2 == 0:
-                    nc.vector.tensor_copy(out=gw[:, 2 * gp : 2 * gp + 2, :, :], in_=bank[:].rearrange("p g u m -> p g m u"))
+                        nc.tensor.transpose(bank[:, which, u, :], words[:, 256 * g + u : 256 * (g + 1) : 2], ident[:])
+                dst = grouped_words[:, 2 * pair : 2 * pair + 2, :, :]
+                src = bank[:].rearrange("p g u m -> p g m u")
+                if (pair + first_engine) % 2 == 0:
+                    nc.vector.tensor_copy(out=dst, in_=src)
                 else:
-                    nc.scalar.copy(out=gw[:, 2 * gp : 2 * gp + 2, :, :], in_=bank[:].rearrange("p g u m -> p g m u"))
-            flat = grp[:].rearrange("p g m k -> p (g m k)")
+                    nc.scalar.copy(out=dst, in_=src)
+            flat = grouped[:].rearrange("p g m k -> p (g m k)")
             lo = 0
-            for width in ((2048, 1024) if passes == 6 else (1024,)):
+            for width in (2048, 1024) if passes == KP1 else (1024,):
                 nc.vector.quantize_mx(
-                    out=cod[:, lo // 4 : (lo + width) // 4].bitcast(FP8X4),
-                    scales=sca[:, lo // 4 : (lo + width) // 4],
+                    out=codes[:, lo // 4 : (lo + width) // 4].bitcast(FP8X4),
+                    scales=scales[:, lo // 4 : (lo + width) // 4],
                     in_=flat[:, lo : lo + width],
                 )
                 lo += width
 
-        w1v = Ws1.rearrange("(g m t) k -> g t m k", g=2, t=4)
+        w1v = Ws1.rearrange("(g m t) k -> g t m k", g=KP2, t=4)
         with tc.tile_pool(name="head", bufs=2) as head:
-            wrows = []
-            for j in range(8):
-                rows = head.tile([P, C], BF16, name="wrow", tag="wrow", bufs=8)
-                nc.sync.dma_start(out=rows[:], in_=w1v[j // 4, j % 4])
-                wrows.append(rows)
+            w_rows = []
+            for j in range(TILES1):
+                w_tile = head.tile([P, C], BF16, name="w1_rows", tag="w1_rows", bufs=TILES1)
+                nc.sync.dma_start(out=w_tile[:], in_=w1v[j // 4, j % 4])
+                w_rows.append(w_tile)
                 if j == 0:
-                    load(0)
-            for h in range(2):
-                rows2 = head.tile([P, HID], BF16, name="wrow2", tag="wrow2", bufs=2)
-                nc.sync.dma_start(out=rows2[:], in_=Ws2[P * h : P * (h + 1), :])
-                wrows.append(rows2)
-            load(1)
-            for j in range(8):
-                turn_weights(head, wrows[j], KP1, w1c[:, j, :], w1s[:, j, :], j)
+                    load_chunk(0)
+            for h in range(MH):
+                w_tile = head.tile([P, HID], BF16, name="w2_rows", tag="w2_rows", bufs=MH)
+                nc.sync.dma_start(out=w_tile[:], in_=Ws2[P * h : P * (h + 1), :])
+                w_rows.append(w_tile)
+            load_chunk(1)
+            for j in range(TILES1):
+                quantize_weights(head, w_rows[j], KP1, w1c[:, j, :], w1s[:, j, :], j)
                 if j == 0:
                     for g in range(KP1):
-                        inter(0, g, g % 2 == 1)
-                        quant(0, g)
-            for h in range(2):
-                turn_weights(head, wrows[8 + h], KP2, w2c[:, h, :], w2s[:, h, :], h)
+                        interleave_x(0, g, g % 2 == 1)
+                        quantize_x(0, g)
+            for h in range(MH):
+                quantize_weights(head, w_rows[TILES1 + h], KP2, w2c[:, h, :], w2s[:, h, :], h)
 
-        pp = ctx.enter_context(tc.tile_pool(name="pp", bufs=20))
-        xtp = ctx.enter_context(tc.tile_pool(name="xtp", bufs=8))
+        pp = ctx.enter_context(tc.tile_pool(name="pp", bufs=MH * (CPI + 2)))
+        xtp = ctx.enter_context(tc.tile_pool(name="xtp", bufs=2 * TPC))
         outp = ctx.enter_context(tc.tile_pool(name="outp", bufs=3))
 
-        hscod = {}
-        pend = []
+        hs_codes = {}
+        hs_waiting = []
 
-        def quant_hs():
-            q, g, grp = pend.pop(0)
-            cod = hsp.tile([P, NCH], U32, name="hcod", tag="hcod", bufs=4, align_bytes=64)
-            sca = hsp.tile([P, NCH], U8, name="hsca", tag="hsca", bufs=4, align_bytes=64)
-            nc.vector.quantize_mx(out=cod[:].bitcast(FP8X4), scales=sca[:], in_=grp[:].rearrange("p n j -> p (n j)"))
-            hscod[(q, g)] = (cod, sca)
+        def quantize_hs():
+            q, group, grouped = hs_waiting.pop(0)
+            codes = hsp.tile([P, NCH], U32, name="hs_codes", tag="hs_codes", bufs=2 * KP2, align_bytes=64)
+            scales = hsp.tile([P, NCH], U8, name="hs_scales", tag="hs_scales", bufs=2 * KP2, align_bytes=64)
+            nc.vector.quantize_mx(
+                out=codes[:].bitcast(FP8X4), scales=scales[:], in_=grouped[:].rearrange("p n j -> p (n j)")
+            )
+            hs_codes[(q, group)] = (codes, scales)
 
-        def on_scalar(q, j):
+        def x_copy_on_scalar(q, j):
             if q < CPI:
                 return j % 2 == 1
-            slot = 8 * (q % CPI) + j
+            slot = TILES1 * (q % CPI) + j
             return PHASES[1][0] <= slot < PHASES[1][1] and slot not in V_IN_SWEEPS
 
         def stage1(q, woven, late):
-            raw = None
-            for j in range(8):
-                g2, t = divmod(j, 4)
+            hs_rows = None
+            for j in range(TILES1):
+                group, t = divmod(j, 4)
                 if j == LAG and late:
                     late.pop(0)()
                 if q + 1 < NQ and j < KP1:
-                    inter(q + 1, j, on_scalar(q, j))
+                    interleave_x(q + 1, j, x_copy_on_scalar(q, j))
                 if q + 1 < NQ and 1 <= j <= KP1:
-                    quant(q + 1, j - 1)
-                if pend and t == 1:
-                    quant_hs()
-                acc = ps1.tile([P, NCH], F32, name="s1", tag="s1")
+                    quantize_x(q + 1, j - 1)
+                if hs_waiting and t == 1:
+                    quantize_hs()
+                bank = ps1.tile([P, NCH], F32, name="stage1", tag="stage1")
                 for g in range(KP1):
-                    cod, sca = xcod[(q, g)]
+                    codes, scales = x_codes[(q, g)]
                     nc.tensor.matmul_mx(
-                        out=acc[:],
+                        out=bank[:],
                         lhsT=w1c[:, j, P * g : P * (g + 1)].bitcast(FP8X4),
                         lhsT_scale=w1s[:, j, P * g : P * (g + 1)],
-                        rhs=cod[:].bitcast(FP8X4),
-                        rhs_scale=sca[:],
+                        rhs=codes[:].bitcast(FP8X4),
+                        rhs_scale=scales[:],
                         start=(g == 0),
                         stop=(g == KP1 - 1),
                     )
                 if t == 0:
-                    raw = hsp.tile([P, 4, NCH], BF16, name="hraw", tag="hraw", bufs=3)
-                nc.scalar.activation(out=raw[:, t, :], in_=acc[:], func=ACT.Relu, bias=b1[:, g2, t : t + 1], scale=1.0)
+                    hs_rows = hsp.tile([P, 4, NCH], BF16, name="hs_rows", tag="hs_rows", bufs=3)
+                nc.scalar.activation(
+                    out=hs_rows[:, t, :], in_=bank[:], func=ACT.Relu, bias=bias[:, group, t : t + 1], scale=1.0
+                )
                 if t == 3:
-                    grp = hsp.tile([P, NCH, 4], BF16, name="hgrp", tag="hgrp", bufs=2, align_bytes=64)
-                    nc.vector.tensor_copy(
-                        out=grp[:].rearrange("p (c i) j -> p c j i", i=4), in_=raw[:].rearrange("p j (c i) -> p c j i", i=4)
-                    )
-                    pend.append((q, g2, grp))
-                for step in woven.pop(8 * q + j, ()):
+                    grouped = hsp.tile([P, NCH, 4], BF16, name="hs_grouped", tag="hs_grouped", bufs=2, align_bytes=64)
+                    dst, src = interleaved(grouped, hs_rows)
+                    nc.vector.tensor_copy(out=dst, in_=src)
+                    hs_waiting.append((q, group, grouped))
+                for step in woven.pop(TILES1 * q + j, ()):
                     step()
             for g in range(KP1):
-                xcod.pop((q, g))
+                x_codes.pop((q, g))
 
-        def stage2(q, pt, mx):
+        def stage2(q, e_tiles, row_max):
             c = q % CPI
-            while pend:
-                quant_hs()
-            for h in range(2):
-                acc = ps2.tile([P, NCH], F32, name="s2", tag="s2")
+            while hs_waiting:
+                quantize_hs()
+            for h in range(MH):
+                bank = ps2.tile([P, NCH], F32, name="stage2", tag="stage2")
                 for g in range(KP2):
-                    cod, sca = hscod[(q, g)]
+                    codes, scales = hs_codes[(q, g)]
                     nc.tensor.matmul_mx(
-                        out=acc[:],
+                        out=bank[:],
                         lhsT=w2c[:, h, P * g : P * (g + 1)].bitcast(FP8X4),
                         lhsT_scale=w2s[:, h, P * g : P * (g + 1)],
-                        rhs=cod[:].bitcast(FP8X4),
-                        rhs_scale=sca[:],
+                        rhs=codes[:].bitcast(FP8X4),
+                        rhs_scale=scales[:],
                         start=(g == 0),
                         stop=(g == KP2 - 1),
                     )
-                t = pp.tile([P, NCH], F32, name="pt", tag="pt")
+                p_tile = pp.tile([P, NCH], F32, name="p_or_e", tag="p_or_e")
                 nc.vector.tensor_scalar(
-                    out=t[:], in0=acc[:], scalar1=1.0, scalar2=None, op0=ALU.mult, op1=ALU.max,
-                    accum_out=mx[:, CPI * h + c : CPI * h + c + 1],
+                    out=p_tile[:], in0=bank[:], scalar1=1.0, scalar2=None, op0=ALU.mult, op1=ALU.max,
+                    accum_out=row_max[:, CPI * h + c : CPI * h + c + 1],
                 )
-                pt[(h, c)] = t
+                e_tiles[(h, c)] = p_tile
             for g in range(KP2):
-                hscod.pop((q, g))
+                hs_codes.pop((q, g))
 
-        def sinkhorn_steps(b, pt, mx, last):
+        def sinkhorn_steps(img, e_tiles, row_max, last):
             s = {}
-            row_pe = TAIL_ROW_PE if last else 0
-            col_pe = TAIL_COL_PE if last else 0
 
             def shift():
-                m2 = small.tile([P, 2], F32, name="m2", tag="m2")
-                nc.vector.tensor_reduce(out=m2[:], in_=mx[:].rearrange("p (h c) -> p h c", h=2), axis=AX.X, op=ALU.max)
-                negm = small.tile([P, 2], F32, name="negm", tag="negm")
-                nc.vector.tensor_scalar(out=negm[:], in0=m2[:], scalar1=-1.0, scalar2=None, op0=ALU.mult)
-                s["negm"] = negm
-                s["r1"] = small.tile([P, 2 * CPI], F32, name="r1", tag="r1")
+                top = small.tile([P, MH], F32, name="top", tag="top")
+                nc.vector.tensor_reduce(
+                    out=top[:], in_=row_max[:].rearrange("p (h c) -> p h c", h=MH), axis=AX.X, op=ALU.max
+                )
+                s["neg_top"] = small.tile([P, MH], F32, name="neg_top", tag="neg_top")
+                nc.vector.tensor_scalar(out=s["neg_top"][:], in0=top[:], scalar1=-1.0, scalar2=None, op0=ALU.mult)
+                s["e_sums"] = small.tile([P, MH * CPI], F32, name="e_sums", tag="e_sums")
 
             def exps(c):
-                for h in range(2):
+                for h in range(MH):
                     nc.scalar.activation(
-                        out=pt[(h, c)][:], in_=pt[(h, c)][:], func=ACT.Exp, bias=s["negm"][:, h : h + 1], scale=1.0,
-                        accum_out=s["r1"][:, CPI * h + c : CPI * h + c + 1],
+                        out=e_tiles[(h, c)][:], in_=e_tiles[(h, c)][:], func=ACT.Exp, bias=s["neg_top"][:, h : h + 1],
+                        scale=1.0, accum_out=s["e_sums"][:, CPI * h + c : CPI * h + c + 1],
                     )
 
             def turn(c):
-                et = xrp.tile([P, 4, M], F32, name="et", tag="k4")
+                et = xrp.tile([P, TPC, M], F32, name="et", tag="x_or_et")
                 s[("et", c)] = et
                 banks = []
-                for half in range(2):
-                    bank = pstr.tile([P, 2, 2, P], F32, name="ebank", tag="tr")
-                    for tt in range(2):
-                        for h in range(2):
-                            lo = P * (2 * half + tt)
-                            nc.tensor.transpose(bank[:, tt, h, :], pt[(h, c)][:, lo : lo + P], ident[:])
+                for pair in range(2):
+                    bank = pstr.tile([P, 2, MH, P], F32, name="e_turned", tag="turned")
+                    for which in range(2):
+                        for h in range(MH):
+                            lo = P * (2 * pair + which)
+                            nc.tensor.transpose(bank[:, which, h, :], e_tiles[(h, c)][:, lo : lo + P], ident[:])
                     banks.append(bank)
-                for half in range(2):
-                    t0 = 2 * half
-                    if last or (half == 0 and c % ET_V == 0):
-                        nc.vector.tensor_copy(out=et[:, t0 : t0 + 2, :], in_=banks[half][:].rearrange("p t h i -> p t (h i)"))
+                for pair in range(2):
+                    dst = et[:, 2 * pair : 2 * pair + 2, :]
+                    src = banks[pair][:].rearrange("p w h i -> p w (h i)")
+                    if last or (pair == 0 and c % 2 == 0):
+                        nc.vector.tensor_copy(out=dst, in_=src)
                     else:
-                        nc.scalar.copy(out=et[:, t0 : t0 + 2, :], in_=banks[half][:].rearrange("p t h i -> p t (h i)"))
+                        nc.scalar.copy(out=dst, in_=src)
 
             def first_a():
-                rc = small.tile([P, 2], F32, name="rc", tag="rc")
-                nc.vector.tensor_reduce(out=rc[:], in_=s["r1"][:].rearrange("p (h c) -> p h c", h=2), axis=AX.X, op=ALU.add)
-                rb = pstr.tile([P, NCH], F32, name="rb", tag="tr")
-                for h in range(2):
+                first_sums = small.tile([P, MH], F32, name="first_sums", tag="first_sums")
+                nc.vector.tensor_reduce(
+                    out=first_sums[:], in_=s["e_sums"][:].rearrange("p (h c) -> p h c", h=MH), axis=AX.X, op=ALU.add
+                )
+                bank = pstr.tile([P, NCH], F32, name="row_sums", tag="turned")
+                for h in range(MH):
                     nc.tensor.matmul(
-                        rb[:, P * h : P * (h + 1)], lhsT=rc[:, h : h + 1].to_broadcast([P, P]), rhs=ident[:],
+                        bank[:, P * h : P * (h + 1)], lhsT=first_sums[:, h : h + 1].to_broadcast([P, P]), rhs=ident[:],
                         start=True, stop=True,
                     )
-                abc = small.tile([P, M + 1], F32, name="abc", tag="abc")
-                nc.vector.reciprocal(out=abc[:, 0:M], in_=rb[:, 0:M])
-                nc.vector.memset(abc[:, M : M + 1], 1.0)
-                s["abc"] = abc
-                if col_pe:
-                    acol = small.tile([P, 2], F32, name="acol", tag="acol")
-                    nc.vector.reciprocal(out=acol[:], in_=rc[:])
-                    s["acol"] = acol
+                a_row = small.tile([P, M + 1], F32, name="a_row", tag="a_row")
+                nc.vector.reciprocal(out=a_row[:, 0:M], in_=bank[:, 0:M])
+                nc.vector.memset(a_row[:, M : M + 1], 1.0)
+                s["a_row"] = a_row
 
-            def col_tensor():
-                cp = pstr.tile([P, NCH], F32, name="cp", tag="tr")
-                for t in range(NT - col_pe, NT):
-                    for h in range(2):
-                        lo = P * (t % 4)
-                        nc.tensor.matmul(
-                            cp[:, t : t + 1], lhsT=pt[(h, t // 4)][:, lo : lo + P], rhs=s["acol"][:, h : h + 1],
-                            start=(h == 0), stop=(h == 1),
-                        )
-                s["cp"] = cp
-
-            def col_part(t0):
-                if t0 == 0:
-                    s["cc"] = small.tile([P, NT], F32, name="cc", tag="cc")
-                for t in range(t0, min(t0 + 4, NT - col_pe)):
-                    nc.vector.scalar_tensor_tensor(
-                        out=junks[t % NJUNK][:], in0=s[("et", t // 4)][:, t % 4, :], scalar=1.0, in1=s["abc"][:, 0:M], op0=ALU.mult, op1=ALU.mult,
-                        accum_out=s["cc"][:, t : t + 1],
-                    )
-
-            def col_end():
-                cd = small.tile([P, NT], F32, name="cd", tag="cd")
-                nv = NT - col_pe
-                nc.vector.tensor_scalar(
-                    out=cd[:, 0:nv], in0=s["cc"][:, 0:nv], scalar1=s["abc"][:, M : M + 1], scalar2=None, op0=ALU.add
-                )
-                if col_pe:
-                    nc.vector.tensor_scalar(
-                        out=cd[:, nv:NT], in0=s["cp"][:, nv:NT], scalar1=s["abc"][:, M : M + 1], scalar2=None, op0=ALU.add
-                    )
-                bb = small.tile([P, NT], F32, name="bb", tag="bb")
-                nc.vector.reciprocal(out=bb[:], in_=cd[:])
-                s["bb"] = bb
-
-            def col_end_part(c):
+            def col_part(c):
                 if c == 0:
-                    s["cd"] = small.tile([P, NT], F32, name="cd", tag="cd")
-                    s["bb"] = small.tile([P, NT], F32, name="bb", tag="bb")
+                    s["col_sums"] = small.tile([P, NT], F32, name="col_sums", tag="col_sums")
+                for pix in range(TPC * c, TPC * (c + 1)):
+                    nc.vector.scalar_tensor_tensor(
+                        out=junks[pix % NJUNK][:], in0=s[("et", c)][:, pix % TPC, :], scalar=1.0, in1=s["a_row"][:, 0:M],
+                        op0=ALU.mult, op1=ALU.mult, accum_out=s["col_sums"][:, pix : pix + 1],
+                    )
+
+            def new_b(lo, hi):
+                if lo == 0:
+                    s["with_dust"] = small.tile([P, NT], F32, name="with_dust", tag="with_dust")
+                    s["b_col"] = small.tile([P, NT], F32, name="b_col", tag="b_col")
                 nc.vector.tensor_scalar(
-                    out=s["cd"][:, 4 * c : 4 * c + 4], in0=s["cc"][:, 4 * c : 4 * c + 4], scalar1=s["abc"][:, M : M + 1],
+                    out=s["with_dust"][:, lo:hi], in0=s["col_sums"][:, lo:hi], scalar1=s["a_row"][:, M : M + 1],
                     scalar2=None, op0=ALU.add,
                 )
-                nc.vector.reciprocal(out=s["bb"][:, 4 * c : 4 * c + 4], in_=s["cd"][:, 4 * c : 4 * c + 4])
+                nc.vector.reciprocal(out=s["b_col"][:, lo:hi], in_=s["with_dust"][:, lo:hi])
 
-            def row_part(t0):
-                et, bb = s[("et", t0 // 4)], s["bb"]
-                if t0 == 0:
+            def row_part(c):
+                et, b_col = s[("et", c)], s["b_col"]
+                if c == 0:
                     nc.vector.tensor_scalar(
-                        out=junk32[:], in0=bb[:], scalar1=1.0 / NPIX, scalar2=None, op0=ALU.mult, op1=ALU.add,
+                        out=junk_b[:], in0=b_col[:], scalar1=1.0 / NPIX, scalar2=None, op0=ALU.mult, op1=ALU.add,
                         accum_out=accs[0][:, M : M + 1],
                     )
-                for t in range(t0, min(t0 + 4, NT - row_pe)):
-                    acc = accs[t % NACC]
-                    if t < NACC:
+                for pix in range(TPC * c, TPC * (c + 1)):
+                    acc = accs[pix % NACC]
+                    if pix < NACC:
                         nc.vector.tensor_scalar(
-                            out=acc[:, 0:M], in0=et[:, t % 4, :], scalar1=bb[:, t : t + 1], scalar2=None, op0=ALU.mult
+                            out=acc[:, 0:M], in0=et[:, pix % TPC, :], scalar1=b_col[:, pix : pix + 1], scalar2=None,
+                            op0=ALU.mult,
                         )
                     else:
                         nc.vector.scalar_tensor_tensor(
-                            out=acc[:, 0:M], in0=et[:, t % 4, :], scalar=bb[:, t : t + 1], in1=acc[:, 0:M],
+                            out=acc[:, 0:M], in0=et[:, pix % TPC, :], scalar=b_col[:, pix : pix + 1], in1=acc[:, 0:M],
                             op0=ALU.mult, op1=ALU.add,
                         )
 
-            def row_end():
-                rb = pstr.tile([P, NCH], F32, name="rb", tag="tr")
-                for k in range(NACC):
-                    nc.tensor.matmul(rb[:, 0 : M + 1], lhsT=ones[:], rhs=accs[k][:], start=(k == 0), stop=(k == NACC - 1))
-                abc = small.tile([P, M + 1], F32, name="abc", tag="abc")
-                nc.vector.reciprocal(out=abc[:], in_=rb[:, 0 : M + 1])
-                s["abc"] = abc
+            def new_a():
+                bank = pstr.tile([P, NCH], F32, name="row_sums", tag="turned")
+                for idx in range(NACC):
+                    nc.tensor.matmul(
+                        bank[:, 0 : M + 1], lhsT=ones[:], rhs=accs[idx][:], start=(idx == 0), stop=(idx == NACC - 1)
+                    )
+                a_row = small.tile([P, M + 1], F32, name="a_row", tag="a_row")
+                nc.vector.reciprocal(out=a_row[:], in_=bank[:, 0 : M + 1])
+                s["a_row"] = a_row
 
-            def a_column():
-                ab = pstr.tile([P, NCH], F32, name="ab", tag="tr")
-                acol = small.tile([P, 2], F32, name="acol", tag="acol")
-                for h in range(2):
-                    nc.tensor.transpose(ab[:, P * h : P * (h + 1)], s["abc"][:, P * h : P * (h + 1)], ident[:])
-                for h in range(2):
-                    nc.vector.tensor_copy(out=acol[:, h : h + 1], in_=ab[:, P * h : P * h + 1])
-                s["acol"] = acol
+            def a_to_column():
+                bank = pstr.tile([P, NCH], F32, name="a_turned", tag="turned")
+                a_col = small.tile([P, MH], F32, name="a_col", tag="a_col")
+                for h in range(MH):
+                    nc.tensor.transpose(bank[:, P * h : P * (h + 1)], s["a_row"][:, P * h : P * (h + 1)], ident[:])
+                for h in range(MH):
+                    nc.vector.tensor_copy(out=a_col[:, h : h + 1], in_=bank[:, P * h : P * h + 1])
+                s["a_col"] = a_col
 
-            def scale_b(c):
-                xts = []
-                for t in range(4 * c, 4 * c + 4):
-                    xt = xtp.tile([P, M], F32, name="xt", tag="xt")
-                    if t % XT_V == 0:
-                        nc.vector.tensor_scalar(
-                            out=xt[:], in0=s[("et", c)][:, t % 4, :], scalar1=s["bb"][:, t : t + 1], scalar2=None, op0=ALU.mult
-                        )
-                    elif XT_G:
-                        nc.gpsimd.tensor_scalar(
-                            out=xt[:], in0=s[("et", c)][:, t % 4, :], scalar1=s["bb"][:, t : t + 1], scalar2=0.0,
-                            op0=ALU.mult, op1=ALU.add,
-                        )
-                    else:
-                        nc.scalar.activation(out=xt[:], in_=s[("et", c)][:, t % 4, :], func=ACT.Copy, scale=s["bb"][:, t : t + 1])
-                    xts.append(xt)
-                s[("xt", c)] = xts
+            def scale_by_b(c):
+                scaled = []
+                for pix in range(TPC * c, TPC * (c + 1)):
+                    scaled_tile = xtp.tile([P, M], F32, name="scaled", tag="scaled")
+                    nc.scalar.activation(
+                        out=scaled_tile[:], in_=s[("et", c)][:, pix % TPC, :], func=ACT.Copy,
+                        scale=s["b_col"][:, pix : pix + 1],
+                    )
+                    scaled.append(scaled_tile)
+                s[("scaled", c)] = scaled
 
             def store(c):
-                xts = s.pop(("xt", c))
+                scaled = s.pop(("scaled", c))
                 banks = []
-                for h in range(2):
+                for h in range(MH):
                     if last:
-                        ob = ps1.tile([P, 4, P], F32, name="ob1", tag="s1")
+                        bank = ps1.tile([P, TPC, P], F32, name="out_turned_last", tag="stage1")
                     else:
-                        ob = pstr.tile([P, 4, P], F32, name="ob", tag="tr")
-                    for tt in range(4):
-                        nc.tensor.transpose(ob[:, tt, :], xts[tt][:, P * h : P * (h + 1)], ident[:])
-                    banks.append(ob)
-                for h in range(2):
+                        bank = pstr.tile([P, TPC, P], F32, name="out_turned", tag="turned")
+                    for sub in range(TPC):
+                        nc.tensor.transpose(bank[:, sub, :], scaled[sub][:, P * h : P * (h + 1)], ident[:])
+                    banks.append(bank)
+                for h in range(MH):
                     if last:
-                        osb = xrp.tile([P, NCH], F32, name="osbl", tag="k4")
+                        result = xrp.tile([P, NCH], F32, name="result_last", tag="x_or_et")
                     else:
-                        osb = outp.tile([P, NCH], F32, name="osb", tag="osb")
-                    if h == 0 and c % (2 if last else OUT_V) == 0:
+                        result = outp.tile([P, NCH], F32, name="result", tag="result")
+                    src = banks[h][:].rearrange("p w n -> p (w n)")
+                    if last and h == 0 and c % 2 == 0:
                         nc.vector.tensor_scalar(
-                            out=osb[:], in0=banks[h][:].rearrange("p t n -> p (t n)"), scalar1=s["acol"][:, h : h + 1],
-                            scalar2=None, op0=ALU.mult,
+                            out=result[:], in0=src, scalar1=s["a_col"][:, h : h + 1], scalar2=None, op0=ALU.mult
                         )
                     else:
-                        nc.scalar.activation(
-                            out=osb[:], in_=banks[h][:].rearrange("p t n -> p (t n)"), func=ACT.Copy, scale=s["acol"][:, h : h + 1]
-                        )
-                    nc.sync.dma_start(out=out[b, P * h : P * (h + 1), NCH * c : NCH * (c + 1)], in_=osb[:])
+                        nc.scalar.activation(out=result[:], in_=src, func=ACT.Copy, scale=s["a_col"][:, h : h + 1])
+                    nc.sync.dma_start(out=out[img, P * h : P * (h + 1), NCH * c : NCH * (c + 1)], in_=result[:])
 
-            def bind(f, arg):
-                return lambda: f(arg)
+            def bind(f, *args):
+                return lambda: f(*args)
+
+            def column_sweep(steps):
+                for c in range(CPI):
+                    steps.append(bind(col_part, c))
+                steps.append(bind(new_b, 0, NT))
 
             prep = [shift, bind(exps, 0)]
             for c in range(1, CPI):
-                prep.append(bind(exps, c))
-                prep.append(bind(turn, c - 1))
-            prep.append(first_a)
-            prep.append(bind(turn, CPI - 1))
+                prep.extend([bind(exps, c), bind(turn, c - 1)])
+            prep.extend([first_a, bind(turn, CPI - 1)])
             sweeps = []
-            for it in range(3):
-                if col_pe:
-                    sweeps.append(col_tensor)
-                for t0 in range(0, NT - col_pe, 4):
-                    sweeps.append(bind(col_part, t0))
-                sweeps.append(col_end)
-                if it < 2:
-                    for t0 in range(0, NT - row_pe, 4):
-                        sweeps.append(bind(row_part, t0))
-                    sweeps.append(row_end)
-                    if col_pe or it == 1:
-                        sweeps.append(a_column)
-            fin = [bind(scale_b, 0)]
-            for c in range(1, CPI):
-                fin.append(bind(scale_b, c))
-                fin.append(bind(store, c - 1))
-            fin.append(bind(store, CPI - 1))
+            for sweep in range(2):
+                column_sweep(sweeps)
+                for c in range(CPI):
+                    sweeps.append(bind(row_part, c))
+                sweeps.append(new_a)
+            sweeps.append(a_to_column)
+            output = []
             if last:
-                sweeps = sweeps[0 : len(sweeps) - CPI - 1]
-                fin = []
                 for c in range(CPI + 2):
                     if c < CPI:
-                        fin.extend([bind(col_part, 4 * c), bind(col_end_part, c)])
+                        output.extend([bind(col_part, c), bind(new_b, TPC * c, TPC * (c + 1))])
                     if 1 <= c <= CPI:
-                        fin.append(bind(scale_b, c - 1))
+                        output.append(bind(scale_by_b, c - 1))
                     if c >= 2:
-                        fin.append(bind(store, c - 2))
-            return (prep, sweeps, fin)
+                        output.append(bind(store, c - 2))
+            else:
+                column_sweep(sweeps)
+                output.append(bind(scale_by_b, 0))
+                for c in range(1, CPI):
+                    output.extend([bind(scale_by_b, c), bind(store, c - 1)])
+                output.append(bind(store, CPI - 1))
+            return (prep, sweeps, output)
 
         def weave(lists, first, woven):
             for steps, (lo, hi) in zip(lists, PHASES):
@@ -467,34 +440,28 @@ def tile_salad_pa_l_kernel(tc, x, Ws1, bs1, Ws2, out):
         state = {}
 
         def second(q):
-            b, c = divmod(q, CPI)
+            img, c = divmod(q, CPI)
             if c == 0:
-                state["pt"] = {}
-                state["mx"] = small.tile([P, 2 * CPI], F32, name="mx", tag="mx")
-            stage2(q, state["pt"], state["mx"])
+                state["e_tiles"] = {}
+                state["row_max"] = small.tile([P, MH * CPI], F32, name="row_max", tag="row_max")
+            stage2(q, state["e_tiles"], state["row_max"])
             if c == CPI - 1:
-                lists = sinkhorn_steps(b, state["pt"], state["mx"], b == B - 1)
-                if b < B - 2:
-                    weave(lists, 8 * (q + 1), woven)
-                elif b == B - 2:
-                    weave(lists[0:2], 8 * (q + 1), woven)
-                    state["held"] = lists[2]
+                prep, sweeps, output = sinkhorn_steps(img, state["e_tiles"], state["row_max"], img == B - 1)
+                if img < B - 2:
+                    weave((prep, sweeps, output), TILES1 * (q + 1), woven)
+                elif img == B - 2:
+                    weave((prep, sweeps), TILES1 * (q + 1), woven)
+                    state["kept"] = output
                 else:
-                    for step in lists[0]:
+                    for step in prep + state["kept"] + sweeps + output:
                         step()
-                    for step in state["held"]:
-                        step()
-                    for steps in lists[1:]:
-                        for step in steps:
-                            step()
 
         def bind_second(q):
             return lambda: second(q)
 
         for q in range(NQ):
-            b, c = divmod(q, CPI)
             if q + 2 < NQ:
-                load(q + 2)
+                load_chunk(q + 2)
             stage1(q, woven, late)
             late.append(bind_second(q))
         for slot in sorted(woven):

from contextlib import ExitStack

import concourse.mybir as mybir
from concourse.masks import make_identity

B, C, NPIX, HID, M = 4, 3072, 4096, 1024, 256
FLOPS = 2 * B * NPIX * (HID * C + M * HID)

F32 = mybir.dt.float32
BF16 = mybir.dt.bfloat16
U32 = mybir.dt.uint32
U8 = mybir.dt.uint8
FP8X4 = mybir.dt.float8_e4m3fn_x4
ALU = mybir.AluOpType
ACT = mybir.ActivationFunctionType
AX = mybir.AxisListType

P = 128
K_PASS = 512
NCH = 512
CPI = NPIX // NCH
NQ = B * CPI
KP1 = C // K_PASS
KP2 = HID // K_PASS
TILES1 = HID // P
MH = M // P
NT = NPIX // P
TPC = NCH // P
NACC = 4
NJUNK = 4
LAG = 3
PHASES = ((4, 13), (13, 59), (59, 68))
V_IN_SWEEPS = (29, 45, 53)


def tile_salad_pa_l_kernel(tc, x, Ws1, bs1, Ws2, out):
    nc = tc.nc
    xv = x.rearrange("b c h w -> b c (h w)")

    with ExitStack() as ctx:
        const = ctx.enter_context(tc.tile_pool(name="const", bufs=1))
        xrp = ctx.enter_context(tc.tile_pool(name="xrp", bufs=16))
        xgp = ctx.enter_context(tc.tile_pool(name="xgp", bufs=3))
        xcp = ctx.enter_context(tc.tile_pool(name="xcp", bufs=2 * KP1))
        hsp = ctx.enter_context(tc.tile_pool(name="hsp", bufs=2))
        small = ctx.enter_context(tc.tile_pool(name="small", bufs=2))
        ps1 = ctx.enter_context(tc.psum_pool(name="ps1", bufs=4))
        ps2 = ctx.enter_context(tc.psum_pool(name="ps2", bufs=MH))
        pstr = ctx.enter_context(tc.psum_pool(name="pstr", bufs=2))

        ident = const.tile([P, P], F32, name="ident")
        make_identity(nc, ident[:])
        ones = const.tile([P, P], F32, name="ones")
        nc.vector.memset(ones[:], 1.0)
        warm = const.tile([P, 1], F32, name="warm")
        nc.scalar.activation(out=warm[:], in_=ones[:, 0:1], func=ACT.Exp)
        bias = const.tile([P, KP2, 4], BF16, name="bias")
        nc.sync.dma_start(out=bias[:], in_=bs1.rearrange("(g p t) -> p g t", g=KP2, t=4))
        w1c = const.tile([P, TILES1, KP1 * P], U32, name="w1c", align_bytes=64)
        w1s = const.tile([P, TILES1, KP1 * P], U8, name="w1s", align_bytes=64)
        w2c = const.tile([P, MH, KP2 * P], U32, name="w2c", align_bytes=64)
        w2s = const.tile([P, MH, KP2 * P], U8, name="w2s", align_bytes=64)
        accs = []
        for idx in range(NACC):
            acc = const.tile([P, M + 1], F32, name="acc%d" % idx)
            nc.vector.memset(acc[:], 0.0)
            accs.append(acc)
        junks = []
        for idx in range(NJUNK):
            junk = const.tile([P, M], BF16, name="junk%d" % idx)
            junks.append(junk)
        junk_b = const.tile([P, NT], F32, name="junk_b")

        def interleaved(grouped, rows):
            return (
                grouped[:].rearrange("p (c i) j -> p c j i", i=4),
                rows[:].rearrange("p j (c i) -> p c j i", i=4),
            )

        x_rows = {}
        x_grouped = {}
        x_codes = {}

        def load_chunk(q):
            img, c = divmod(q, CPI)
            for g in range(KP1):
                x_tile = xrp.tile([P, 4, NCH], BF16, name="x_rows", tag="x_or_et")
                nc.sync.dma_start(
                    out=x_tile[:],
                    in_=xv[img, K_PASS * g : K_PASS * (g + 1), NCH * c : NCH * (c + 1)].rearrange("(p j) n -> p j n", j=4),
                )
                x_rows[(q, g)] = x_tile

        def interleave_x(q, g, on_scalar):
            grouped = xgp.tile([P, NCH, 4], BF16, name="x_grouped", tag="x_grouped", align_bytes=64)
            dst, src = interleaved(grouped, x_rows.pop((q, g)))
            if on_scalar:
                nc.scalar.copy(out=dst, in_=src)
            else:
                nc.vector.tensor_copy(out=dst, in_=src)
            x_grouped[(q, g)] = grouped

        def quantize_x(q, g):
            grouped = x_grouped.pop((q, g))
            codes = xcp.tile([P, NCH], U32, name="x_codes", tag="x_codes", align_bytes=64)
            scales = xcp.tile([P, NCH], U8, name="x_scales", tag="x_scales", align_bytes=64)
            nc.vector.quantize_mx(
                out=codes[:].bitcast(FP8X4), scales=scales[:], in_=grouped[:].rearrange("p n j -> p (n j)")
            )
            x_codes[(q, g)] = (codes, scales)

        def quantize_weights(head, w_tile, passes, codes, scales, first_engine):
            words = w_tile[:].bitcast(F32)
            grouped = head.tile([P, KP1, P, 4], BF16, name="w_grouped", tag="w_grouped", bufs=1, align_bytes=64)
            grouped_words = grouped[:].bitcast(F32)
            for pair in range(passes // 2):
                bank = pstr.tile([P, 2, 2, P], F32, name="w_turned", tag="turned")
                for which in range(2):
                    g = 2 * pair + which
                    for u in range(2):
                        nc.tensor.transpose(bank[:, which, u, :], words[:, 256 * g + u : 256 * (g + 1) : 2], ident[:])
                dst = grouped_words[:, 2 * pair : 2 * pair + 2, :, :]
                src = bank[:].rearrange("p g u m -> p g m u")
                if (pair + first_engine) % 2 == 0:
                    nc.vector.tensor_copy(out=dst, in_=src)
                else:
                    nc.scalar.copy(out=dst, in_=src)
            flat = grouped[:].rearrange("p g m k -> p (g m k)")
            lo = 0
            for width in (2048, 1024) if passes == KP1 else (1024,):
                nc.vector.quantize_mx(
                    out=codes[:, lo // 4 : (lo + width) // 4].bitcast(FP8X4),
                    scales=scales[:, lo // 4 : (lo + width) // 4],
                    in_=flat[:, lo : lo + width],
                )
                lo += width

        w1v = Ws1.rearrange("(g m t) k -> g t m k", g=KP2, t=4)
        with tc.tile_pool(name="head", bufs=2) as head:
            w_rows = []
            for j in range(TILES1):
                w_tile = head.tile([P, C], BF16, name="w1_rows", tag="w1_rows", bufs=TILES1)
                nc.sync.dma_start(out=w_tile[:], in_=w1v[j // 4, j % 4])
                w_rows.append(w_tile)
                if j == 0:
                    load_chunk(0)
            for h in range(MH):
                w_tile = head.tile([P, HID], BF16, name="w2_rows", tag="w2_rows", bufs=MH)
                nc.sync.dma_start(out=w_tile[:], in_=Ws2[P * h : P * (h + 1), :])
                w_rows.append(w_tile)
            load_chunk(1)
            for j in range(TILES1):
                quantize_weights(head, w_rows[j], KP1, w1c[:, j, :], w1s[:, j, :], j)
                if j == 0:
                    for g in range(KP1):
                        interleave_x(0, g, g % 2 == 1)
                        quantize_x(0, g)
            for h in range(MH):
                quantize_weights(head, w_rows[TILES1 + h], KP2, w2c[:, h, :], w2s[:, h, :], h)

        pp = ctx.enter_context(tc.tile_pool(name="pp", bufs=MH * (CPI + 2)))
        xtp = ctx.enter_context(tc.tile_pool(name="xtp", bufs=2 * TPC))
        outp = ctx.enter_context(tc.tile_pool(name="outp", bufs=3))

        hs_codes = {}
        hs_waiting = []

        def quantize_hs():
            q, group, grouped = hs_waiting.pop(0)
            codes = hsp.tile([P, NCH], U32, name="hs_codes", tag="hs_codes", bufs=2 * KP2, align_bytes=64)
            scales = hsp.tile([P, NCH], U8, name="hs_scales", tag="hs_scales", bufs=2 * KP2, align_bytes=64)
            nc.vector.quantize_mx(
                out=codes[:].bitcast(FP8X4), scales=scales[:], in_=grouped[:].rearrange("p n j -> p (n j)")
            )
            hs_codes[(q, group)] = (codes, scales)

        def x_copy_on_scalar(q, j):
            if q < CPI:
                return j % 2 == 1
            slot = TILES1 * (q % CPI) + j
            return PHASES[1][0] <= slot < PHASES[1][1] and slot not in V_IN_SWEEPS

        def stage1(q, woven, late):
            hs_rows = None
            for j in range(TILES1):
                group, t = divmod(j, 4)
                if j == LAG and late:
                    late.pop(0)()
                if q + 1 < NQ and j < KP1:
                    interleave_x(q + 1, j, x_copy_on_scalar(q, j))
                if q + 1 < NQ and 1 <= j <= KP1:
                    quantize_x(q + 1, j - 1)
                if hs_waiting and t == 1:
                    quantize_hs()
                bank = ps1.tile([P, NCH], F32, name="stage1", tag="stage1")
                for g in range(KP1):
                    codes, scales = x_codes[(q, g)]
                    nc.tensor.matmul_mx(
                        out=bank[:],
                        lhsT=w1c[:, j, P * g : P * (g + 1)].bitcast(FP8X4),
                        lhsT_scale=w1s[:, j, P * g : P * (g + 1)],
                        rhs=codes[:].bitcast(FP8X4),
                        rhs_scale=scales[:],
                        start=(g == 0),
                        stop=(g == KP1 - 1),
                    )
                if t == 0:
                    hs_rows = hsp.tile([P, 4, NCH], BF16, name="hs_rows", tag="hs_rows", bufs=3)
                nc.scalar.activation(
                    out=hs_rows[:, t, :], in_=bank[:], func=ACT.Relu, bias=bias[:, group, t : t + 1], scale=1.0
                )
                if t == 3:
                    grouped = hsp.tile([P, NCH, 4], BF16, name="hs_grouped", tag="hs_grouped", bufs=2, align_bytes=64)
                    dst, src = interleaved(grouped, hs_rows)
                    nc.vector.tensor_copy(out=dst, in_=src)
                    hs_waiting.append((q, group, grouped))
                for step in woven.pop(TILES1 * q + j, ()):
                    step()
            for g in range(KP1):
                x_codes.pop((q, g))

        def stage2(q, e_tiles, row_max):
            c = q % CPI
            while hs_waiting:
                quantize_hs()
            for h in range(MH):
                bank = ps2.tile([P, NCH], F32, name="stage2", tag="stage2")
                for g in range(KP2):
                    codes, scales = hs_codes[(q, g)]
                    nc.tensor.matmul_mx(
                        out=bank[:],
                        lhsT=w2c[:, h, P * g : P * (g + 1)].bitcast(FP8X4),
                        lhsT_scale=w2s[:, h, P * g : P * (g + 1)],
                        rhs=codes[:].bitcast(FP8X4),
                        rhs_scale=scales[:],
                        start=(g == 0),
                        stop=(g == KP2 - 1),
                    )
                p_tile = pp.tile([P, NCH], F32, name="p_or_e", tag="p_or_e")
                nc.vector.tensor_scalar(
                    out=p_tile[:], in0=bank[:], scalar1=1.0, scalar2=None, op0=ALU.mult, op1=ALU.max,
                    accum_out=row_max[:, CPI * h + c : CPI * h + c + 1],
                )
                e_tiles[(h, c)] = p_tile
            for g in range(KP2):
                hs_codes.pop((q, g))

        def sinkhorn_steps(img, e_tiles, row_max, last):
            s = {}

            def shift():
                top = small.tile([P, MH], F32, name="top", tag="top")
                nc.vector.tensor_reduce(
                    out=top[:], in_=row_max[:].rearrange("p (h c) -> p h c", h=MH), axis=AX.X, op=ALU.max
                )
                s["neg_top"] = small.tile([P, MH], F32, name="neg_top", tag="neg_top")
                nc.vector.tensor_scalar(out=s["neg_top"][:], in0=top[:], scalar1=-1.0, scalar2=None, op0=ALU.mult)
                s["e_sums"] = small.tile([P, MH * CPI], F32, name="e_sums", tag="e_sums")

            def exps(c):
                for h in range(MH):
                    nc.scalar.activation(
                        out=e_tiles[(h, c)][:], in_=e_tiles[(h, c)][:], func=ACT.Exp, bias=s["neg_top"][:, h : h + 1],
                        scale=1.0, accum_out=s["e_sums"][:, CPI * h + c : CPI * h + c + 1],
                    )

            def turn(c):
                et = xrp.tile([P, TPC, M], F32, name="et", tag="x_or_et")
                s[("et", c)] = et
                banks = []
                for pair in range(2):
                    bank = pstr.tile([P, 2, MH, P], F32, name="e_turned", tag="turned")
                    for which in range(2):
                        for h in range(MH):
                            lo = P * (2 * pair + which)
                            nc.tensor.transpose(bank[:, which, h, :], e_tiles[(h, c)][:, lo : lo + P], ident[:])
                    banks.append(bank)
                for pair in range(2):
                    dst = et[:, 2 * pair : 2 * pair + 2, :]
                    src = banks[pair][:].rearrange("p w h i -> p w (h i)")
                    if last or (pair == 0 and c % 2 == 0):
                        nc.vector.tensor_copy(out=dst, in_=src)
                    else:
                        nc.scalar.copy(out=dst, in_=src)

            def first_a():
                first_sums = small.tile([P, MH], F32, name="first_sums", tag="first_sums")
                nc.vector.tensor_reduce(
                    out=first_sums[:], in_=s["e_sums"][:].rearrange("p (h c) -> p h c", h=MH), axis=AX.X, op=ALU.add
                )
                bank = pstr.tile([P, NCH], F32, name="row_sums", tag="turned")
                for h in range(MH):
                    nc.tensor.matmul(
                        bank[:, P * h : P * (h + 1)], lhsT=first_sums[:, h : h + 1].to_broadcast([P, P]), rhs=ident[:],
                        start=True, stop=True,
                    )
                a_row = small.tile([P, M + 1], F32, name="a_row", tag="a_row")
                nc.vector.reciprocal(out=a_row[:, 0:M], in_=bank[:, 0:M])
                nc.vector.memset(a_row[:, M : M + 1], 1.0)
                s["a_row"] = a_row

            def col_part(c):
                if c == 0:
                    s["col_sums"] = small.tile([P, NT], F32, name="col_sums", tag="col_sums")
                for pix in range(TPC * c, TPC * (c + 1)):
                    nc.vector.scalar_tensor_tensor(
                        out=junks[pix % NJUNK][:], in0=s[("et", c)][:, pix % TPC, :], scalar=1.0, in1=s["a_row"][:, 0:M],
                        op0=ALU.mult, op1=ALU.mult, accum_out=s["col_sums"][:, pix : pix + 1],
                    )

            def new_b(lo, hi):
                if lo == 0:
                    s["with_dust"] = small.tile([P, NT], F32, name="with_dust", tag="with_dust")
                    s["b_col"] = small.tile([P, NT], F32, name="b_col", tag="b_col")
                nc.vector.tensor_scalar(
                    out=s["with_dust"][:, lo:hi], in0=s["col_sums"][:, lo:hi], scalar1=s["a_row"][:, M : M + 1],
                    scalar2=None, op0=ALU.add,
                )
                nc.vector.reciprocal(out=s["b_col"][:, lo:hi], in_=s["with_dust"][:, lo:hi])

            def row_part(c):
                et, b_col = s[("et", c)], s["b_col"]
                if c == 0:
                    nc.vector.tensor_scalar(
                        out=junk_b[:], in0=b_col[:], scalar1=1.0 / NPIX, scalar2=None, op0=ALU.mult, op1=ALU.add,
                        accum_out=accs[0][:, M : M + 1],
                    )
                for pix in range(TPC * c, TPC * (c + 1)):
                    acc = accs[pix % NACC]
                    if pix < NACC:
                        nc.vector.tensor_scalar(
                            out=acc[:, 0:M], in0=et[:, pix % TPC, :], scalar1=b_col[:, pix : pix + 1], scalar2=None,
                            op0=ALU.mult,
                        )
                    else:
                        nc.vector.scalar_tensor_tensor(
                            out=acc[:, 0:M], in0=et[:, pix % TPC, :], scalar=b_col[:, pix : pix + 1], in1=acc[:, 0:M],
                            op0=ALU.mult, op1=ALU.add,
                        )

            def new_a():
                bank = pstr.tile([P, NCH], F32, name="row_sums", tag="turned")
                for idx in range(NACC):
                    nc.tensor.matmul(
                        bank[:, 0 : M + 1], lhsT=ones[:], rhs=accs[idx][:], start=(idx == 0), stop=(idx == NACC - 1)
                    )
                a_row = small.tile([P, M + 1], F32, name="a_row", tag="a_row")
                nc.vector.reciprocal(out=a_row[:], in_=bank[:, 0 : M + 1])
                s["a_row"] = a_row

            def a_to_column():
                bank = pstr.tile([P, NCH], F32, name="a_turned", tag="turned")
                a_col = small.tile([P, MH], F32, name="a_col", tag="a_col")
                for h in range(MH):
                    nc.tensor.transpose(bank[:, P * h : P * (h + 1)], s["a_row"][:, P * h : P * (h + 1)], ident[:])
                for h in range(MH):
                    nc.vector.tensor_copy(out=a_col[:, h : h + 1], in_=bank[:, P * h : P * h + 1])
                s["a_col"] = a_col

            def scale_by_b(c):
                scaled = []
                for pix in range(TPC * c, TPC * (c + 1)):
                    scaled_tile = xtp.tile([P, M], F32, name="scaled", tag="scaled")
                    nc.scalar.activation(
                        out=scaled_tile[:], in_=s[("et", c)][:, pix % TPC, :], func=ACT.Copy,
                        scale=s["b_col"][:, pix : pix + 1],
                    )
                    scaled.append(scaled_tile)
                s[("scaled", c)] = scaled

            def store(c):
                scaled = s.pop(("scaled", c))
                banks = []
                for h in range(MH):
                    if last:
                        bank = ps1.tile([P, TPC, P], F32, name="out_turned_last", tag="stage1")
                    else:
                        bank = pstr.tile([P, TPC, P], F32, name="out_turned", tag="turned")
                    for sub in range(TPC):
                        nc.tensor.transpose(bank[:, sub, :], scaled[sub][:, P * h : P * (h + 1)], ident[:])
                    banks.append(bank)
                for h in range(MH):
                    if last:
                        result = xrp.tile([P, NCH], F32, name="result_last", tag="x_or_et")
                    else:
                        result = outp.tile([P, NCH], F32, name="result", tag="result")
                    src = banks[h][:].rearrange("p w n -> p (w n)")
                    if last and h == 0 and c % 2 == 0:
                        nc.vector.tensor_scalar(
                            out=result[:], in0=src, scalar1=s["a_col"][:, h : h + 1], scalar2=None, op0=ALU.mult
                        )
                    else:
                        nc.scalar.activation(out=result[:], in_=src, func=ACT.Copy, scale=s["a_col"][:, h : h + 1])
                    nc.sync.dma_start(out=out[img, P * h : P * (h + 1), NCH * c : NCH * (c + 1)], in_=result[:])

            def bind(f, *args):
                return lambda: f(*args)

            def column_sweep(steps):
                for c in range(CPI):
                    steps.append(bind(col_part, c))
                steps.append(bind(new_b, 0, NT))

            prep = [shift, bind(exps, 0)]
            for c in range(1, CPI):
                prep.extend([bind(exps, c), bind(turn, c - 1)])
            prep.extend([first_a, bind(turn, CPI - 1)])
            sweeps = []
            for sweep in range(2):
                column_sweep(sweeps)
                for c in range(CPI):
                    sweeps.append(bind(row_part, c))
                sweeps.append(new_a)
            sweeps.append(a_to_column)
            output = []
            if last:
                for c in range(CPI + 2):
                    if c < CPI:
                        output.extend([bind(col_part, c), bind(new_b, TPC * c, TPC * (c + 1))])
                    if 1 <= c <= CPI:
                        output.append(bind(scale_by_b, c - 1))
                    if c >= 2:
                        output.append(bind(store, c - 2))
            else:
                column_sweep(sweeps)
                output.append(bind(scale_by_b, 0))
                for c in range(1, CPI):
                    output.extend([bind(scale_by_b, c), bind(store, c - 1)])
                output.append(bind(store, CPI - 1))
            return (prep, sweeps, output)

        def weave(lists, first, woven):
            for steps, (lo, hi) in zip(lists, PHASES):
                for i, step in enumerate(steps):
                    slot = first + lo + (i * (hi - lo)) // len(steps)
                    woven[slot] = woven.get(slot, []) + [step]

        woven = {}
        late = []
        state = {}

        def second(q):
            img, c = divmod(q, CPI)
            if c == 0:
                state["e_tiles"] = {}
                state["row_max"] = small.tile([P, MH * CPI], F32, name="row_max", tag="row_max")
            stage2(q, state["e_tiles"], state["row_max"])
            if c == CPI - 1:
                prep, sweeps, output = sinkhorn_steps(img, state["e_tiles"], state["row_max"], img == B - 1)
                if img < B - 2:
                    weave((prep, sweeps, output), TILES1 * (q + 1), woven)
                elif img == B - 2:
                    weave((prep, sweeps), TILES1 * (q + 1), woven)
                    state["kept"] = output
                else:
                    for step in prep + state["kept"] + sweeps + output:
                        step()

        def bind_second(q):
            return lambda: second(q)

        for q in range(NQ):
            if q + 2 < NQ:
                load_chunk(q + 2)
            stage1(q, woven, late)
            late.append(bind_second(q))
        for slot in sorted(woven):
            for step in woven[slot]:
                step()
        late.pop(0)()
